import numpy as np
import ml_dtypes


def mxq(x, axis, fmt="e4m3"):
    dtype, down = {"e4m3": (ml_dtypes.float8_e4m3fn, 7), "e5m2": (ml_dtypes.float8_e5m2, 14)}[fmt]
    v = np.moveaxis(np.asarray(x, np.float32).astype(ml_dtypes.bfloat16).astype(np.float64), axis, -1)
    blocks = v.reshape(v.shape[:-1] + (-1, 32))
    amax = np.abs(blocks).max(-1, keepdims=True)
    byte = np.maximum(np.where(amax > 0, np.frexp(amax)[1] - 1 + 127, 0) - down, 1)
    scale = np.exp2(byte - 127.0)
    codes = (blocks / scale).astype(np.float32).astype(dtype).astype(np.float64)
    return np.moveaxis((codes * scale).reshape(v.shape), -1, axis)


BF16 = ml_dtypes.bfloat16


def bf(x):
    return np.asarray(x, np.float32).astype(BF16)


def f64(x):
    return np.asarray(x).astype(np.float64)


B, D_IN, H1, H2, H3, C = 1024, 2048, 2048, 2048, 1024, 1024
BN_EPS = 1e-5


def binarize(w):
    return np.where(w >= 0, 1.0, -1.0)


def bn_relu(z, gamma, beta):
    m = z.mean(axis=0)
    v = z.var(axis=0)
    return np.maximum((z - m) * (1.0 / np.sqrt(v + BN_EPS)) * gamma + beta, 0.0)


def setup_inputs():
    c = 4.0 * np.exp2(-12.0 * np.random.random(H1))
    mu = 0.5 * np.random.standard_normal(H1)
    return {"z0": bf((np.random.standard_normal((B, H1)) + mu) * c),
            "g0": bf(0.25 * (1.0 + 0.1 * np.random.standard_normal(H1))),
            "beta0": bf(0.1 * np.random.standard_normal(H1)),
            "Wb1": bf(np.random.standard_normal((H2, H1)) / np.sqrt(H1)),
            "bb1": bf(np.random.standard_normal(H2))}


def reference(z0, g0, beta0, Wb1, bb1):
    h = bn_relu(f64(z0), f64(g0), f64(beta0))
    ws = binarize(f64(Wb1))
    return (mxq(h, 1, "e4m3") @ mxq(ws, 1, "e4m3").T) + f64(bb1)

@@ -1,0 +1,208 @@
+from contextlib import ExitStack
+
+import concourse.mybir as mybir
+from concourse.masks import make_identity
+
+F32 = mybir.dt.float32
+BF16 = mybir.dt.bfloat16
+U32 = mybir.dt.uint32
+U8 = mybir.dt.uint8
+FP8X4 = mybir.dt.float8_e4m3fn_x4
+ALU = mybir.AluOpType
+ACT = mybir.ActivationFunctionType
+
+P = 128
+PACK = 4
+K_PASS = P * PACK
+BATCH = 1024
+K = 2048
+N = 2048
+PASSES = K // K_PASS
+ROW_TILES = BATCH // P
+N_TILE = 512
+N_TILES = N // N_TILE
+W_ROWS = 256
+W_LOADS = N // W_ROWS
+BN_CHUNK = 512
+BN_EPS = 1e-5
+
+SIGN_SCALE = 2.0**64
+SIGN_BIAS = 2.0**-100
+
+FLOPS = 2 * BATCH * K * N
+
+
+def tile_binarymlp_pa_kernel(tc, z0, g0, beta0, Wb1, bb1, out):
+    nc = tc.nc
+    with ExitStack() as ctx:
+        const = ctx.enter_context(tc.tile_pool(name="const", bufs=1))
+        inputs = ctx.enter_context(tc.tile_pool(name="inputs", bufs=1))
+        keep = ctx.enter_context(tc.tile_pool(name="keep", bufs=1))
+        small = ctx.enter_context(tc.tile_pool(name="small", bufs=4))
+        h_stage = ctx.enter_context(tc.tile_pool(name="h_stage", bufs=2))
+        w_stage = ctx.enter_context(tc.tile_pool(name="w_stage", bufs=3))
+        o_stage = ctx.enter_context(tc.tile_pool(name="o_stage", bufs=4))
+        tr_psum = ctx.enter_context(tc.psum_pool(name="tr_psum", bufs=4))
+        acc_psum = ctx.enter_context(tc.psum_pool(name="acc_psum", bufs=4))
+
+        ident_bf = const.tile([P, P], BF16)
+        make_identity(nc, ident_bf[:])
+        ident_f32 = const.tile([P, P], F32)
+        make_identity(nc, ident_f32[:])
+        neg_half = const.tile([P, 1], F32)
+        nc.gpsimd.memset(neg_half[:], -0.5)
+
+        gain = const.tile([P, K // P], BF16)
+        shift = const.tile([P, K // P], BF16)
+        with nc.allow_non_contiguous_dma(reason="two small vectors, in pairs of elements"):
+            nc.scalar.dma_start(
+                out=gain[:].rearrange("p (c e) -> p c e", e=2),
+                in_=g0.rearrange("(c p e) -> p c e", p=P, e=2),
+            )
+            nc.scalar.dma_start(
+                out=shift[:].rearrange("p (c e) -> p c e", e=2),
+                in_=beta0.rearrange("(c p e) -> p c e", p=P, e=2),
+            )
+
+        z_sb = [inputs.tile([P, ROW_TILES, K_PASS], BF16, name="z_sb%d" % g) for g in range(PASSES)]
+        w_sb = [inputs.tile([P, W_ROWS // P, K], BF16, name="w_sb%d" % c) for c in range(W_LOADS)]
+
+        def load_z(g):
+            nc.sync.dma_start(
+                out=z_sb[g][:],
+                in_=z0[:, g * K_PASS : (g + 1) * K_PASS].rearrange("(r p) c -> p r c", p=P),
+            )
+
+        def load_w(c):
+            nc.sync.dma_start(
+                out=w_sb[c][:],
+                in_=Wb1[c * W_ROWS : (c + 1) * W_ROWS, :].rearrange("(i p) k -> p i k", p=P),
+            )
+
+        load_z(0)
+        for g in range(1, PASSES):
+            load_z(g)
+            load_w(2 * g - 2)
+            load_w(2 * g - 1)
+        for c in range(2 * PASSES - 2, W_LOADS):
+            load_w(c)
+        bias_bc = const.tile([P, N], BF16)
+        nc.sync.dma_start(out=bias_bc[:], in_=bb1.partition_broadcast(P))
+
+        h_codes = keep.tile([P, PASSES, BATCH], U32, align_bytes=64)
+        h_scales = keep.tile([P, PASSES, BATCH], U8, align_bytes=64)
+        w_codes = keep.tile([P, PASSES, N], U32, align_bytes=64)
+        w_scales = keep.tile([P, PASSES, N], U8, align_bytes=64)
+
+        def normalise_block(g, t, h_t):
+            u, e = divmod(t, 2)
+            feature = PACK * g + t
+            columns = z_sb[g][:].rearrange("p r (u q e) -> p r u e q", u=2, e=2)
+            z_t = tr_psum.tile([P, BATCH], BF16, tag="tr")
+            for r in range(ROW_TILES):
+                nc.tensor.transpose(z_t[:, r * P : (r + 1) * P], columns[:, r, u, e, :], ident_bf[:])
+            stats = small.tile([P, BATCH // BN_CHUNK, 6], F32)
+            for c in range(BATCH // BN_CHUNK):
+                nc.vector.bn_stats(out=stats[:, c, :], in_=z_t[:, c * BN_CHUNK : (c + 1) * BN_CHUNK])
+            mean_var = small.tile([P, 2], F32)
+            nc.vector.bn_aggr(out=mean_var[:], in_=stats[:].rearrange("p c s -> p (c s)"))
+            var_eps = small.tile([P, 1], F32)
+            nc.gpsimd.tensor_scalar(
+                out=var_eps[:], in0=mean_var[:, 1:2], scalar1=BN_EPS, scalar2=None, op0=ALU.add
+            )
+            rstd = small.tile([P, 1], F32)
+            nc.gpsimd.tensor_tensor(out=rstd[:], in0=var_eps[:], in1=neg_half[:], op=ALU.pow)
+            scale = small.tile([P, 1], F32)
+            nc.gpsimd.tensor_tensor(
+                out=scale[:], in0=rstd[:], in1=gain[:, feature : feature + 1], op=ALU.mult
+            )
+            mean_scaled = small.tile([P, 1], F32)
+            nc.gpsimd.tensor_tensor(
+                out=mean_scaled[:], in0=mean_var[:, 0:1], in1=scale[:], op=ALU.mult
+            )
+            offset = small.tile([P, 1], F32)
+            nc.gpsimd.tensor_tensor(
+                out=offset[:], in0=shift[:, feature : feature + 1], in1=mean_scaled[:], op=ALU.subtract
+            )
+            nc.scalar.activation(
+                out=h_t[:, t, :], in_=z_t[:], func=ACT.Relu, bias=offset[:], scale=scale[:]
+            )
+
+        def quantise_h(g, h_t):
+            h_grouped = h_stage.tile([P, BATCH, PACK], BF16, align_bytes=64)
+            for half in range(2):
+                rows = slice(half * (BATCH // 2), (half + 1) * (BATCH // 2))
+                nc.vector.tensor_copy(
+                    out=h_grouped[:, rows, :].rearrange("p (c i) t -> p c t i", i=4),
+                    in_=h_t[:, :, rows].rearrange("p t (c i) -> p c t i", i=4),
+                )
+            nc.vector.quantize_mx(
+                out=h_codes[:, g, :].bitcast(FP8X4),
+                scales=h_scales[:, g, :],
+                in_=h_grouped[:].rearrange("p b t -> p (b t)"),
+            )
+
+        w_grouped_of = {}
+
+        def binarise_half(index):
+            piece, s = divmod(index, 2)
+            j, g = divmod(piece, PASSES)
+            if s == 0:
+                w_grouped_of[piece] = w_stage.tile([P, N_TILE, PACK], BF16, align_bytes=64, name="w_grouped")
+            w_grouped = w_grouped_of[piece]
+            words = w_sb[2 * j + s][:].bitcast(F32)
+            w_t = tr_psum.tile([P, 2, W_ROWS], F32, tag="tr")
+            for u in range(2):
+                first = (K_PASS // 2) * g + P * u
+                for i in range(W_ROWS // P):
+                    nc.tensor.transpose(
+                        w_t[:, u, i * P : (i + 1) * P], words[:, i, first : first + P], ident_f32[:]
+                    )
+            nc.scalar.activation(
+                out=w_grouped[:, s * W_ROWS : (s + 1) * W_ROWS, :].rearrange("p r (u e) -> p r u e", e=2),
+                in_=w_t[:].bitcast(BF16).rearrange("p u (r e) -> p r u e", e=2),
+                func=ACT.Sign,
+                bias=SIGN_BIAS,
+                scale=SIGN_SCALE,
+            )
+            if s == 1:
+                n_cols = slice(j * N_TILE, (j + 1) * N_TILE)
+                nc.vector.quantize_mx(
+                    out=w_codes[:, g, n_cols].bitcast(FP8X4),
+                    scales=w_scales[:, g, n_cols],
+                    in_=w_grouped[:].rearrange("p r t -> p (r t)"),
+                )
+
+        def out_tile(j, m):
+            m_cols = slice(m * P, (m + 1) * P)
+            n_cols = slice(j * N_TILE, (j + 1) * N_TILE)
+            acc = acc_psum.tile([P, N_TILE], F32)
+            for g in range(PASSES):
+                nc.tensor.matmul_mx(
+                    out=acc[:],
+                    lhsT=h_codes[:, g, m_cols].bitcast(FP8X4),
+                    lhsT_scale=h_scales[:, g, m_cols],
+                    rhs=w_codes[:, g, n_cols].bitcast(FP8X4),
+                    rhs_scale=w_scales[:, g, n_cols],
+                    start=(g == 0),
+                    stop=(g == PASSES - 1),
+                )
+            result = o_stage.tile([P, N_TILE], F32)
+            nc.vector.tensor_tensor(out=result[:], in0=acc[:], in1=bias_bc[:, n_cols], op=ALU.add)
+            nc.sync.dma_start(out=out[m_cols, n_cols], in_=result[:])
+
+        for g in range(PASSES):
+            h_t = h_stage.tile([P, PACK, BATCH], BF16)
+            for t in range(PACK):
+                normalise_block(g, t, h_t)
+                binarise_half(PACK * g + t)
+            quantise_h(g, h_t)
+
+        halves_done = PACK * PASSES
+        for j in range(N_TILES):
+            for m in range(ROW_TILES):
+                if m % 2 == 0 and halves_done < 2 * PASSES * N_TILES:
+                    binarise_half(halves_done)
+                    binarise_half(halves_done + 1)
+                    halves_done += 2
+                out_tile(j, m)

@@ -19,12 +19,17 @@ K = 2048
 N = 2048
 PASSES = K // K_PASS
 ROW_TILES = BATCH // P
+HALF = BATCH // 2
 N_TILE = 512
 N_TILES = N // N_TILE
 W_ROWS = 256
 W_LOADS = N // W_ROWS
+W_UNITS = W_LOADS * PASSES
+UNITS_PER_N_TILE = W_UNITS // N_TILES
 BN_CHUNK = 512
 BN_EPS = 1e-5
+LEAD = 2
+UNIT_RUN = 4
 
 SIGN_SCALE = 2.0**64
 SIGN_BIAS = 2.0**-100
@@ -35,21 +40,21 @@ FLOPS = 2 * BATCH * K * N
 def tile_binarymlp_pa_kernel(tc, z0, g0, beta0, Wb1, bb1, out):
     nc = tc.nc
     with ExitStack() as ctx:
+        ctx.enter_context(tc.manual_schedule())
         const = ctx.enter_context(tc.tile_pool(name="const", bufs=1))
         inputs = ctx.enter_context(tc.tile_pool(name="inputs", bufs=1))
         keep = ctx.enter_context(tc.tile_pool(name="keep", bufs=1))
         small = ctx.enter_context(tc.tile_pool(name="small", bufs=4))
         h_stage = ctx.enter_context(tc.tile_pool(name="h_stage", bufs=2))
-        w_stage = ctx.enter_context(tc.tile_pool(name="w_stage", bufs=3))
+        w_stage = ctx.enter_context(tc.tile_pool(name="w_stage", bufs=UNIT_RUN))
         o_stage = ctx.enter_context(tc.tile_pool(name="o_stage", bufs=4))
-        tr_psum = ctx.enter_context(tc.psum_pool(name="tr_psum", bufs=4))
-        acc_psum = ctx.enter_context(tc.psum_pool(name="acc_psum", bufs=4))
+        w_psum = ctx.enter_context(tc.psum_pool(name="w_psum", bufs=UNIT_RUN))
 
         ident_bf = const.tile([P, P], BF16)
         make_identity(nc, ident_bf[:])
         ident_f32 = const.tile([P, P], F32)
         make_identity(nc, ident_f32[:])
-        neg_half = const.tile([P, 1], F32)
+        neg_half = const.tile([P, PACK], F32)
         nc.gpsimd.memset(neg_half[:], -0.5)
 
         gain = const.tile([P, K // P], BF16)
@@ -80,11 +85,12 @@ def tile_binarymlp_pa_kernel(tc, z0, g0, beta0, Wb1, bb1, out):
             )
 
         load_z(0)
-        for g in range(1, PASSES):
-            load_z(g)
-            load_w(2 * g - 2)
-            load_w(2 * g - 1)
-        for c in range(2 * PASSES - 2, W_LOADS):
+        load_w(0)
+        load_z(1)
+        load_w(1)
+        load_z(2)
+        load_z(3)
+        for c in range(2, W_LOADS):
             load_w(c)
         bias_bc = const.tile([P, N], BF16)
         nc.sync.dma_start(out=bias_bc[:], in_=bb1.partition_broadcast(P))
@@ -94,86 +100,102 @@ def tile_binarymlp_pa_kernel(tc, z0, g0, beta0, Wb1, bb1, out):
         w_codes = keep.tile([P, PASSES, N], U32, align_bytes=64)
         w_scales = keep.tile([P, PASSES, N], U8, align_bytes=64)
 
-        def normalise_block(g, t, h_t):
+        def transpose_features(g, t, z_t):
             u, e = divmod(t, 2)
-            feature = PACK * g + t
             columns = z_sb[g][:].rearrange("p r (u q e) -> p r u e q", u=2, e=2)
-            z_t = tr_psum.tile([P, BATCH], BF16, tag="tr")
             for r in range(ROW_TILES):
                 nc.tensor.transpose(z_t[:, r * P : (r + 1) * P], columns[:, r, u, e, :], ident_bf[:])
+
+        mean_var_of = {}
+        scale_of = {}
+        offset_of = {}
+        h_t_of = {}
+        w_grouped_of = {}
+
+        def statistics(g, t, stats_psum):
+            if t == 0:
+                mean_var_of[g] = small.tile([P, PACK, 2], F32, name="mean_var")
+            z_t = stats_psum.tile([P, BATCH], BF16, name="z_t_stats")
+            transpose_features(g, t, z_t)
             stats = small.tile([P, BATCH // BN_CHUNK, 6], F32)
             for c in range(BATCH // BN_CHUNK):
                 nc.vector.bn_stats(out=stats[:, c, :], in_=z_t[:, c * BN_CHUNK : (c + 1) * BN_CHUNK])
-            mean_var = small.tile([P, 2], F32)
-            nc.vector.bn_aggr(out=mean_var[:], in_=stats[:].rearrange("p c s -> p (c s)"))
-            var_eps = small.tile([P, 1], F32)
-            nc.gpsimd.tensor_scalar(
-                out=var_eps[:], in0=mean_var[:, 1:2], scalar1=BN_EPS, scalar2=None, op0=ALU.add
-            )
-            rstd = small.tile([P, 1], F32)
+            nc.vector.bn_aggr(out=mean_var_of[g][:, t, :], in_=stats[:].rearrange("p c s -> p (c s)"))
+
+        def scale_and_offset(g):
+            features = slice(PACK * g, PACK * (g + 1))
+            mean = mean_var_of[g][:, :, 0]
+            var = mean_var_of[g][:, :, 1]
+            var_eps = small.tile([P, PACK], F32)
+            nc.gpsimd.tensor_scalar(out=var_eps[:], in0=var, scalar1=BN_EPS, scalar2=None, op0=ALU.add)
+            rstd = small.tile([P, PACK], F32)
             nc.gpsimd.tensor_tensor(out=rstd[:], in0=var_eps[:], in1=neg_half[:], op=ALU.pow)
-            scale = small.tile([P, 1], F32)
+            scale_of[g] = small.tile([P, PACK], F32, name="scale")
+            nc.gpsimd.tensor_tensor(out=scale_of[g][:], in0=rstd[:], in1=gain[:, features], op=ALU.mult)
+            mean_scaled = small.tile([P, PACK], F32)
+            nc.gpsimd.tensor_tensor(out=mean_scaled[:], in0=mean, in1=scale_of[g][:], op=ALU.mult)
+            offset_of[g] = small.tile([P, PACK], F32, name="offset")
             nc.gpsimd.tensor_tensor(
-                out=scale[:], in0=rstd[:], in1=gain[:, feature : feature + 1], op=ALU.mult
-            )
-            mean_scaled = small.tile([P, 1], F32)
-            nc.gpsimd.tensor_tensor(
-                out=mean_scaled[:], in0=mean_var[:, 0:1], in1=scale[:], op=ALU.mult
-            )
-            offset = small.tile([P, 1], F32)
-            nc.gpsimd.tensor_tensor(
-                out=offset[:], in0=shift[:, feature : feature + 1], in1=mean_scaled[:], op=ALU.subtract
-            )
-            nc.scalar.activation(
-                out=h_t[:, t, :], in_=z_t[:], func=ACT.Relu, bias=offset[:], scale=scale[:]
+                out=offset_of[g][:], in0=shift[:, features], in1=mean_scaled[:], op=ALU.subtract
             )
 
-        def quantise_h(g, h_t):
+        def norm_relu(g, t, norm_psum):
+            if t == 0:
+                h_t_of[g] = h_stage.tile([P, PACK, BATCH], BF16, name="h_t")
+            z_t = norm_psum.tile([P, BATCH], BF16, name="z_t_norm")
+            transpose_features(g, t, z_t)
+            nc.scalar.activation(
+                out=h_t_of[g][:, t, :],
+                in_=z_t[:],
+                func=ACT.Relu,
+                bias=offset_of[g][:, t : t + 1],
+                scale=scale_of[g][:, t : t + 1],
+            )
+
+        def quantise_h(g):
             h_grouped = h_stage.tile([P, BATCH, PACK], BF16, align_bytes=64)
-            for half in range(2):
-                rows = slice(half * (BATCH // 2), (half + 1) * (BATCH // 2))
+            halves = [slice(first, first + HALF) for first in range(0, BATCH, HALF)]
+            for rows in halves:
                 nc.vector.tensor_copy(
                     out=h_grouped[:, rows, :].rearrange("p (c i) t -> p c t i", i=4),
-                    in_=h_t[:, :, rows].rearrange("p t (c i) -> p c t i", i=4),
+                    in_=h_t_of[g][:, :, rows].rearrange("p t (c i) -> p c t i", i=4),
                 )
-            nc.vector.quantize_mx(
-                out=h_codes[:, g, :].bitcast(FP8X4),
-                scales=h_scales[:, g, :],
-                in_=h_grouped[:].rearrange("p b t -> p (b t)"),
-            )
+            for rows in halves:
+                nc.vector.quantize_mx(
+                    out=h_codes[:, g, rows].bitcast(FP8X4),
+                    scales=h_scales[:, g, rows],
+                    in_=h_grouped[:, rows, :].rearrange("p b t -> p (b t)"),
+                )
 
-        w_grouped_of = {}
-
-        def binarise_half(index):
-            piece, s = divmod(index, 2)
-            j, g = divmod(piece, PASSES)
-            if s == 0:
-                w_grouped_of[piece] = w_stage.tile([P, N_TILE, PACK], BF16, align_bytes=64, name="w_grouped")
-            w_grouped = w_grouped_of[piece]
-            words = w_sb[2 * j + s][:].bitcast(F32)
-            w_t = tr_psum.tile([P, 2, W_ROWS], F32, tag="tr")
+        def binarise(unit):
+            c, g = divmod(unit, PASSES)
+            words = w_sb[c][:].bitcast(F32)
+            w_t = w_psum.tile([P, 2, W_ROWS], F32)
             for u in range(2):
                 first = (K_PASS // 2) * g + P * u
                 for i in range(W_ROWS // P):
                     nc.tensor.transpose(
                         w_t[:, u, i * P : (i + 1) * P], words[:, i, first : first + P], ident_f32[:]
                     )
+            w_grouped_of[unit] = w_stage.tile([P, W_ROWS, PACK], BF16, align_bytes=64, name="w_grouped")
             nc.scalar.activation(
-                out=w_grouped[:, s * W_ROWS : (s + 1) * W_ROWS, :].rearrange("p r (u e) -> p r u e", e=2),
+                out=w_grouped_of[unit][:].rearrange("p r (u e) -> p r u e", e=2),
                 in_=w_t[:].bitcast(BF16).rearrange("p u (r e) -> p r u e", e=2),
                 func=ACT.Sign,
                 bias=SIGN_BIAS,
                 scale=SIGN_SCALE,
             )
-            if s == 1:
-                n_cols = slice(j * N_TILE, (j + 1) * N_TILE)
-                nc.vector.quantize_mx(
-                    out=w_codes[:, g, n_cols].bitcast(FP8X4),
-                    scales=w_scales[:, g, n_cols],
-                    in_=w_grouped[:].rearrange("p r t -> p (r t)"),
-                )
 
-        def out_tile(j, m):
+        def quantise_w(unit):
+            c, g = divmod(unit, PASSES)
+            n_cols = slice(c * W_ROWS, (c + 1) * W_ROWS)
+            nc.vector.quantize_mx(
+                out=w_codes[:, g, n_cols].bitcast(FP8X4),
+                scales=w_scales[:, g, n_cols],
+                in_=w_grouped_of[unit][:].rearrange("p r t -> p (r t)"),
+            )
+
+        def out_tile(j, m, acc_psum):
             m_cols = slice(m * P, (m + 1) * P)
             n_cols = slice(j * N_TILE, (j + 1) * N_TILE)
             acc = acc_psum.tile([P, N_TILE], F32)
@@ -191,18 +213,37 @@ def tile_binarymlp_pa_kernel(tc, z0, g0, beta0, Wb1, bb1, out):
             nc.vector.tensor_tensor(out=result[:], in0=acc[:], in1=bias_bc[:, n_cols], op=ALU.add)
             nc.sync.dma_start(out=out[m_cols, n_cols], in_=result[:])
 
-        for g in range(PASSES):
-            h_t = h_stage.tile([P, PACK, BATCH], BF16)
-            for t in range(PACK):
-                normalise_block(g, t, h_t)
-                binarise_half(PACK * g + t)
-            quantise_h(g, h_t)
+        with ExitStack() as stage:
+            stats_psum = stage.enter_context(tc.psum_pool(name="stats_psum", bufs=2))
+            norm_psum = stage.enter_context(tc.psum_pool(name="norm_psum", bufs=2))
+            for step in range((PASSES + LEAD) * PACK):
+                ahead, t = divmod(step, PACK)
+                g = ahead - LEAD
+                if ahead < PASSES:
+                    statistics(ahead, t, stats_psum)
+                    if t == PACK - 1:
+                        scale_and_offset(ahead)
+                if g >= 0:
+                    norm_relu(g, t, norm_psum)
+                unit = step - 1
+                if 0 <= unit < UNITS_PER_N_TILE:
+                    binarise(unit)
+                if 0 <= unit - 1 < UNITS_PER_N_TILE:
+                    quantise_w(unit - 1)
+                if g >= 1 and t == 1:
+                    quantise_h(g - 1)
+            quantise_h(PASSES - 1)
 
-        halves_done = PACK * PASSES
-        for j in range(N_TILES):
-            for m in range(ROW_TILES):
-                if m % 2 == 0 and halves_done < 2 * PASSES * N_TILES:
-                    binarise_half(halves_done)
-                    binarise_half(halves_done + 1)
-                    halves_done += 2
-                out_tile(j, m)
+        with tc.psum_pool(name="acc_psum", bufs=4, reuse_waits="tile") as acc_psum:
+            binarised = UNITS_PER_N_TILE
+            quantised = UNITS_PER_N_TILE
+            for j in range(N_TILES):
+                for m in range(ROW_TILES):
+                    if m % UNIT_RUN == 0 and binarised < W_UNITS:
+                        for unit in range(binarised, binarised + UNIT_RUN):
+                            binarise(unit)
+                        binarised += UNIT_RUN
+                    out_tile(j, m, acc_psum)
+                    if quantised < binarised:
+                        quantise_w(quantised)
+                        quantised += 1

@@ -28,7 +28,11 @@ W_UNITS = W_LOADS * PASSES
 UNITS_PER_N_TILE = W_UNITS // N_TILES
 BN_CHUNK = 512
 BN_EPS = 1e-5
-LEAD = 2
+PAIRS = K // (2 * P)
+PSUM_BANKS = 8
+Z_BANKS = 6
+NORM_LAG = 2
+QUANT_LAG = 2
 UNIT_RUN = 4
 
 SIGN_SCALE = 2.0**64
@@ -48,13 +52,12 @@ def tile_binarymlp_pa_kernel(tc, z0, g0, beta0, Wb1, bb1, out):
         h_stage = ctx.enter_context(tc.tile_pool(name="h_stage", bufs=2))
         w_stage = ctx.enter_context(tc.tile_pool(name="w_stage", bufs=UNIT_RUN))
         o_stage = ctx.enter_context(tc.tile_pool(name="o_stage", bufs=4))
-        w_psum = ctx.enter_context(tc.psum_pool(name="w_psum", bufs=UNIT_RUN))
 
         ident_bf = const.tile([P, P], BF16)
         make_identity(nc, ident_bf[:])
         ident_f32 = const.tile([P, P], F32)
         make_identity(nc, ident_f32[:])
-        neg_half = const.tile([P, PACK], F32)
+        neg_half = const.tile([P, 2], F32)
         nc.gpsimd.memset(neg_half[:], -0.5)
 
         gain = const.tile([P, K // P], BF16)
@@ -100,57 +103,55 @@ def tile_binarymlp_pa_kernel(tc, z0, g0, beta0, Wb1, bb1, out):
         w_codes = keep.tile([P, PASSES, N], U32, align_bytes=64)
         w_scales = keep.tile([P, PASSES, N], U8, align_bytes=64)
 
-        def transpose_features(g, t, z_t):
-            u, e = divmod(t, 2)
-            columns = z_sb[g][:].rearrange("p r (u q e) -> p r u e q", u=2, e=2)
-            for r in range(ROW_TILES):
-                nc.tensor.transpose(z_t[:, r * P : (r + 1) * P], columns[:, r, u, e, :], ident_bf[:])
-
-        mean_var_of = {}
+        z_t_of = {}
         scale_of = {}
         offset_of = {}
         h_t_of = {}
         w_grouped_of = {}
 
-        def statistics(g, t, stats_psum):
-            if t == 0:
-                mean_var_of[g] = small.tile([P, PACK, 2], F32, name="mean_var")
-            z_t = stats_psum.tile([P, BATCH], BF16, name="z_t_stats")
-            transpose_features(g, t, z_t)
+        def statistics(pair, e, mean_var, z_psum):
+            g, u = divmod(pair, 2)
+            columns = z_sb[g][:].rearrange("p r (u q e) -> p r u e q", u=2, e=2)
+            z_t = z_psum.tile([P, BATCH], BF16)
+            for r in range(ROW_TILES):
+                nc.tensor.transpose(z_t[:, r * P : (r + 1) * P], columns[:, r, u, e, :], ident_bf[:])
             stats = small.tile([P, BATCH // BN_CHUNK, 6], F32)
             for c in range(BATCH // BN_CHUNK):
                 nc.vector.bn_stats(out=stats[:, c, :], in_=z_t[:, c * BN_CHUNK : (c + 1) * BN_CHUNK])
-            nc.vector.bn_aggr(out=mean_var_of[g][:, t, :], in_=stats[:].rearrange("p c s -> p (c s)"))
+            nc.vector.bn_aggr(out=mean_var[:, e, :], in_=stats[:].rearrange("p c s -> p (c s)"))
+            z_t_of[(pair, e)] = z_t
 
-        def scale_and_offset(g):
-            features = slice(PACK * g, PACK * (g + 1))
-            mean = mean_var_of[g][:, :, 0]
-            var = mean_var_of[g][:, :, 1]
-            var_eps = small.tile([P, PACK], F32)
-            nc.gpsimd.tensor_scalar(out=var_eps[:], in0=var, scalar1=BN_EPS, scalar2=None, op0=ALU.add)
-            rstd = small.tile([P, PACK], F32)
+        def scale_and_offset(pair, mean_var):
+            features = slice(2 * pair, 2 * pair + 2)
+            var_eps = small.tile([P, 2], F32)
+            nc.gpsimd.tensor_scalar(
+                out=var_eps[:], in0=mean_var[:, :, 1], scalar1=BN_EPS, scalar2=None, op0=ALU.add
+            )
+            rstd = small.tile([P, 2], F32)
             nc.gpsimd.tensor_tensor(out=rstd[:], in0=var_eps[:], in1=neg_half[:], op=ALU.pow)
-            scale_of[g] = small.tile([P, PACK], F32, name="scale")
-            nc.gpsimd.tensor_tensor(out=scale_of[g][:], in0=rstd[:], in1=gain[:, features], op=ALU.mult)
-            mean_scaled = small.tile([P, PACK], F32)
-            nc.gpsimd.tensor_tensor(out=mean_scaled[:], in0=mean, in1=scale_of[g][:], op=ALU.mult)
-            offset_of[g] = small.tile([P, PACK], F32, name="offset")
+            scale_of[pair] = small.tile([P, 2], F32, name="scale")
+            nc.gpsimd.tensor_tensor(out=scale_of[pair][:], in0=rstd[:], in1=gain[:, features], op=ALU.mult)
+            mean_scaled = small.tile([P, 2], F32)
             nc.gpsimd.tensor_tensor(
-                out=offset_of[g][:], in0=shift[:, features], in1=mean_scaled[:], op=ALU.subtract
+                out=mean_scaled[:], in0=mean_var[:, :, 0], in1=scale_of[pair][:], op=ALU.mult
+            )
+            offset_of[pair] = small.tile([P, 2], F32, name="offset")
+            nc.gpsimd.tensor_tensor(
+                out=offset_of[pair][:], in0=shift[:, features], in1=mean_scaled[:], op=ALU.subtract
             )
 
-        def norm_relu(g, t, norm_psum):
-            if t == 0:
+        def norm_relu(pair):
+            g, u = divmod(pair, 2)
+            if u == 0:
                 h_t_of[g] = h_stage.tile([P, PACK, BATCH], BF16, name="h_t")
-            z_t = norm_psum.tile([P, BATCH], BF16, name="z_t_norm")
-            transpose_features(g, t, z_t)
-            nc.scalar.activation(
-                out=h_t_of[g][:, t, :],
-                in_=z_t[:],
-                func=ACT.Relu,
-                bias=offset_of[g][:, t : t + 1],
-                scale=scale_of[g][:, t : t + 1],
-            )
+            for e in range(2):
+                nc.scalar.activation(
+                    out=h_t_of[g][:, 2 * u + e, :],
+                    in_=z_t_of[(pair, e)][:],
+                    func=ACT.Relu,
+                    bias=offset_of[pair][:, e : e + 1],
+                    scale=scale_of[pair][:, e : e + 1],
+                )
 
         def quantise_h(g):
             h_grouped = h_stage.tile([P, BATCH, PACK], BF16, align_bytes=64)
@@ -167,7 +168,7 @@ def tile_binarymlp_pa_kernel(tc, z0, g0, beta0, Wb1, bb1, out):
                     in_=h_grouped[:, rows, :].rearrange("p b t -> p (b t)"),
                 )
 
-        def binarise(unit):
+        def binarise(unit, w_psum):
             c, g = divmod(unit, PASSES)
             words = w_sb[c][:].bitcast(F32)
             w_t = w_psum.tile([P, 2, W_ROWS], F32)
@@ -214,34 +215,35 @@ def tile_binarymlp_pa_kernel(tc, z0, g0, beta0, Wb1, bb1, out):
             nc.sync.dma_start(out=out[m_cols, n_cols], in_=result[:])
 
         with ExitStack() as stage:
-            stats_psum = stage.enter_context(tc.psum_pool(name="stats_psum", bufs=2))
-            norm_psum = stage.enter_context(tc.psum_pool(name="norm_psum", bufs=2))
-            for step in range((PASSES + LEAD) * PACK):
-                ahead, t = divmod(step, PACK)
-                g = ahead - LEAD
-                if ahead < PASSES:
-                    statistics(ahead, t, stats_psum)
-                    if t == PACK - 1:
-                        scale_and_offset(ahead)
-                if g >= 0:
-                    norm_relu(g, t, norm_psum)
-                unit = step - 1
-                if 0 <= unit < UNITS_PER_N_TILE:
-                    binarise(unit)
-                if 0 <= unit - 1 < UNITS_PER_N_TILE:
-                    quantise_w(unit - 1)
-                if g >= 1 and t == 1:
-                    quantise_h(g - 1)
-            quantise_h(PASSES - 1)
+            z_psum = stage.enter_context(tc.psum_pool(name="z_psum", bufs=Z_BANKS))
+            w_psum = stage.enter_context(tc.psum_pool(name="w_psum_first", bufs=PSUM_BANKS - Z_BANKS))
+            for step in range(PAIRS + NORM_LAG + QUANT_LAG):
+                if 0 <= step - NORM_LAG < PAIRS:
+                    norm_relu(step - NORM_LAG)
+                if step < PAIRS:
+                    mean_var = small.tile([P, 2, 2], F32)
+                    for e in range(2):
+                        statistics(step, e, mean_var, z_psum)
+                        unit = 2 * step + e - 1
+                        if 0 <= unit < UNITS_PER_N_TILE:
+                            binarise(unit, w_psum)
+                        if 0 <= unit - 2 < UNITS_PER_N_TILE:
+                            quantise_w(unit - 2)
+                    scale_and_offset(step, mean_var)
+                g, u = divmod(step - NORM_LAG - QUANT_LAG, 2)
+                if g >= 0 and u == 1:
+                    quantise_h(g)
 
-        with tc.psum_pool(name="acc_psum", bufs=4, reuse_waits="tile") as acc_psum:
+        with ExitStack() as stage:
+            acc_psum = stage.enter_context(tc.psum_pool(name="acc_psum", bufs=4, reuse_waits="tile"))
+            w_psum = stage.enter_context(tc.psum_pool(name="w_psum_second", bufs=UNIT_RUN, reuse_waits="tile"))
             binarised = UNITS_PER_N_TILE
             quantised = UNITS_PER_N_TILE
             for j in range(N_TILES):
                 for m in range(ROW_TILES):
                     if m % UNIT_RUN == 0 and binarised < W_UNITS:
                         for unit in range(binarised, binarised + UNIT_RUN):
-                            binarise(unit)
+                            binarise(unit, w_psum)
                         binarised += UNIT_RUN
                     out_tile(j, m, acc_psum)
                     if quantised < binarised:

@@ -51,7 +51,7 @@ def tile_binarymlp_pa_kernel(tc, z0, g0, beta0, Wb1, bb1, out):
         small = ctx.enter_context(tc.tile_pool(name="small", bufs=4))
         h_stage = ctx.enter_context(tc.tile_pool(name="h_stage", bufs=2))
         w_stage = ctx.enter_context(tc.tile_pool(name="w_stage", bufs=UNIT_RUN))
-        o_stage = ctx.enter_context(tc.tile_pool(name="o_stage", bufs=4))
+        o_stage = ctx.enter_context(tc.tile_pool(name="o_stage", bufs=6))
 
         ident_bf = const.tile([P, P], BF16)
         make_identity(nc, ident_bf[:])
@@ -60,25 +60,22 @@ def tile_binarymlp_pa_kernel(tc, z0, g0, beta0, Wb1, bb1, out):
         neg_half = const.tile([P, 2], F32)
         nc.gpsimd.memset(neg_half[:], -0.5)
 
-        gain = const.tile([P, K // P], BF16)
-        shift = const.tile([P, K // P], BF16)
-        with nc.allow_non_contiguous_dma(reason="two small vectors, in pairs of elements"):
-            nc.scalar.dma_start(
-                out=gain[:].rearrange("p (c e) -> p c e", e=2),
-                in_=g0.rearrange("(c p e) -> p c e", p=P, e=2),
-            )
-            nc.scalar.dma_start(
-                out=shift[:].rearrange("p (c e) -> p c e", e=2),
-                in_=beta0.rearrange("(c p e) -> p c e", p=P, e=2),
-            )
+        vec_rows = const.tile([P, P], F32)
+        nc.vector.memset(vec_rows[:], 0.0)
+        nc.scalar.dma_start(
+            out=vec_rows[0:PAIRS, :].bitcast(BF16), in_=g0.rearrange("(c w) -> c w", c=PAIRS)
+        )
+        nc.scalar.dma_start(
+            out=vec_rows[PAIRS : 2 * PAIRS, :].bitcast(BF16), in_=beta0.rearrange("(c w) -> c w", c=PAIRS)
+        )
 
-        z_sb = [inputs.tile([P, ROW_TILES, K_PASS], BF16, name="z_sb%d" % g) for g in range(PASSES)]
+        z_sb = [inputs.tile([P, ROW_TILES, 2 * P], BF16, name="z_sb%d" % pair) for pair in range(PAIRS)]
         w_sb = [inputs.tile([P, W_ROWS // P, K], BF16, name="w_sb%d" % c) for c in range(W_LOADS)]
 
-        def load_z(g):
+        def load_z(pair):
             nc.sync.dma_start(
-                out=z_sb[g][:],
-                in_=z0[:, g * K_PASS : (g + 1) * K_PASS].rearrange("(r p) c -> p r c", p=P),
+                out=z_sb[pair][:],
+                in_=z0[:, pair * 2 * P : (pair + 1) * 2 * P].rearrange("(r p) c -> p r c", p=P),
             )
 
         def load_w(c):
@@ -87,13 +84,13 @@ def tile_binarymlp_pa_kernel(tc, z0, g0, beta0, Wb1, bb1, out):
                 in_=Wb1[c * W_ROWS : (c + 1) * W_ROWS, :].rearrange("(i p) k -> p i k", p=P),
             )
 
-        load_z(0)
-        load_w(0)
-        load_z(1)
-        load_w(1)
-        load_z(2)
-        load_z(3)
-        for c in range(2, W_LOADS):
+        for c in range(N_TILE // W_ROWS):
+            load_z(2 * c)
+            load_z(2 * c + 1)
+            load_w(c)
+        for pair in range(2 * (N_TILE // W_ROWS), PAIRS):
+            load_z(pair)
+        for c in range(N_TILE // W_ROWS, W_LOADS):
             load_w(c)
         bias_bc = const.tile([P, N], BF16)
         nc.sync.dma_start(out=bias_bc[:], in_=bb1.partition_broadcast(P))
@@ -109,20 +106,25 @@ def tile_binarymlp_pa_kernel(tc, z0, g0, beta0, Wb1, bb1, out):
         h_t_of = {}
         w_grouped_of = {}
 
-        def statistics(pair, e, mean_var, z_psum):
-            g, u = divmod(pair, 2)
-            columns = z_sb[g][:].rearrange("p r (u q e) -> p r u e q", u=2, e=2)
-            z_t = z_psum.tile([P, BATCH], BF16)
-            for r in range(ROW_TILES):
-                nc.tensor.transpose(z_t[:, r * P : (r + 1) * P], columns[:, r, u, e, :], ident_bf[:])
-            stats = small.tile([P, BATCH // BN_CHUNK, 6], F32)
-            for c in range(BATCH // BN_CHUNK):
-                nc.vector.bn_stats(out=stats[:, c, :], in_=z_t[:, c * BN_CHUNK : (c + 1) * BN_CHUNK])
-            nc.vector.bn_aggr(out=mean_var[:, e, :], in_=stats[:].rearrange("p c s -> p (c s)"))
-            z_t_of[(pair, e)] = z_t
+        def statistics(pair, mean_var, z_psum):
+            columns = z_sb[pair][:].rearrange("p r (q e) -> p r e q", e=2)
+            for e in range(2):
+                z_t = z_psum.tile([P, BATCH], BF16)
+                for r in range(ROW_TILES):
+                    nc.tensor.transpose(z_t[:, r * P : (r + 1) * P], columns[:, r, e, :], ident_bf[:])
+                z_t_of[(pair, e)] = z_t
+            stats = small.tile([P, 2, BATCH // BN_CHUNK, 6], F32)
+            for e in range(2):
+                for c in range(BATCH // BN_CHUNK):
+                    nc.vector.bn_stats(
+                        out=stats[:, e, c, :], in_=z_t_of[(pair, e)][:, c * BN_CHUNK : (c + 1) * BN_CHUNK]
+                    )
+            for e in range(2):
+                nc.vector.bn_aggr(out=mean_var[:, e, :], in_=stats[:, e, :, :].rearrange("p c s -> p (c s)"))
 
-        def scale_and_offset(pair, mean_var):
-            features = slice(2 * pair, 2 * pair + 2)
+        def scale_and_offset(pair, mean_var, gain_shift):
+            gain = gain_shift[:, pair : pair + 1].bitcast(BF16)
+            shift = gain_shift[:, PAIRS + pair : PAIRS + pair + 1].bitcast(BF16)
             var_eps = small.tile([P, 2], F32)
             nc.gpsimd.tensor_scalar(
                 out=var_eps[:], in0=mean_var[:, :, 1], scalar1=BN_EPS, scalar2=None, op0=ALU.add
@@ -130,14 +132,14 @@ def tile_binarymlp_pa_kernel(tc, z0, g0, beta0, Wb1, bb1, out):
             rstd = small.tile([P, 2], F32)
             nc.gpsimd.tensor_tensor(out=rstd[:], in0=var_eps[:], in1=neg_half[:], op=ALU.pow)
             scale_of[pair] = small.tile([P, 2], F32, name="scale")
-            nc.gpsimd.tensor_tensor(out=scale_of[pair][:], in0=rstd[:], in1=gain[:, features], op=ALU.mult)
+            nc.gpsimd.tensor_tensor(out=scale_of[pair][:], in0=rstd[:], in1=gain, op=ALU.mult)
             mean_scaled = small.tile([P, 2], F32)
             nc.gpsimd.tensor_tensor(
                 out=mean_scaled[:], in0=mean_var[:, :, 0], in1=scale_of[pair][:], op=ALU.mult
             )
             offset_of[pair] = small.tile([P, 2], F32, name="offset")
             nc.gpsimd.tensor_tensor(
-                out=offset_of[pair][:], in0=shift[:, features], in1=mean_scaled[:], op=ALU.subtract
+                out=offset_of[pair][:], in0=shift, in1=mean_scaled[:], op=ALU.subtract
             )
 
         def norm_relu(pair):
@@ -217,19 +219,22 @@ def tile_binarymlp_pa_kernel(tc, z0, g0, beta0, Wb1, bb1, out):
         with ExitStack() as stage:
             z_psum = stage.enter_context(tc.psum_pool(name="z_psum", bufs=Z_BANKS))
             w_psum = stage.enter_context(tc.psum_pool(name="w_psum_first", bufs=PSUM_BANKS - Z_BANKS))
+            vec_t = w_psum.tile([P, P], F32, tag="w_t")
+            nc.tensor.transpose(vec_t[:], vec_rows[:], ident_f32[:])
+            gain_shift = const.tile([P, 2 * PAIRS], F32)
+            nc.vector.tensor_copy(out=gain_shift[:], in_=vec_t[:, 0 : 2 * PAIRS])
             for step in range(PAIRS + NORM_LAG + QUANT_LAG):
                 if 0 <= step - NORM_LAG < PAIRS:
                     norm_relu(step - NORM_LAG)
                 if step < PAIRS:
                     mean_var = small.tile([P, 2, 2], F32)
-                    for e in range(2):
-                        statistics(step, e, mean_var, z_psum)
-                        unit = 2 * step + e - 1
-                        if 0 <= unit < UNITS_PER_N_TILE:
-                            binarise(unit, w_psum)
-                        if 0 <= unit - 2 < UNITS_PER_N_TILE:
-                            quantise_w(unit - 2)
-                    scale_and_offset(step, mean_var)
+                    statistics(step, mean_var, z_psum)
+                    scale_and_offset(step, mean_var, gain_shift)
+                for unit in range(2 * (step - 1), 2 * step):
+                    if 0 <= unit < UNITS_PER_N_TILE:
+                        binarise(unit, w_psum)
+                    if 0 <= unit - 2 < UNITS_PER_N_TILE:
+                        quantise_w(unit - 2)
                 g, u = divmod(step - NORM_LAG - QUANT_LAG, 2)
                 if g >= 0 and u == 1:
                     quantise_h(g)

@@ -34,6 +34,7 @@ Z_BANKS = 6
 NORM_LAG = 2
 QUANT_LAG = 2
 UNIT_RUN = 4
+UNIT_EVERY = 3
 
 SIGN_SCALE = 2.0**64
 SIGN_BIAS = 2.0**-100
@@ -219,16 +220,17 @@ def tile_binarymlp_pa_kernel(tc, z0, g0, beta0, Wb1, bb1, out):
         with ExitStack() as stage:
             z_psum = stage.enter_context(tc.psum_pool(name="z_psum", bufs=Z_BANKS))
             w_psum = stage.enter_context(tc.psum_pool(name="w_psum_first", bufs=PSUM_BANKS - Z_BANKS))
-            vec_t = w_psum.tile([P, P], F32, tag="w_t")
-            nc.tensor.transpose(vec_t[:], vec_rows[:], ident_f32[:])
             gain_shift = const.tile([P, 2 * PAIRS], F32)
-            nc.vector.tensor_copy(out=gain_shift[:], in_=vec_t[:, 0 : 2 * PAIRS])
             for step in range(PAIRS + NORM_LAG + QUANT_LAG):
                 if 0 <= step - NORM_LAG < PAIRS:
                     norm_relu(step - NORM_LAG)
                 if step < PAIRS:
                     mean_var = small.tile([P, 2, 2], F32)
                     statistics(step, mean_var, z_psum)
+                    if step == 0:
+                        vec_t = w_psum.tile([P, P], F32, tag="w_t")
+                        nc.tensor.transpose(vec_t[:], vec_rows[:], ident_f32[:])
+                        nc.vector.tensor_copy(out=gain_shift[:], in_=vec_t[:, 0 : 2 * PAIRS])
                     scale_and_offset(step, mean_var, gain_shift)
                 for unit in range(2 * (step - 1), 2 * step):
                     if 0 <= unit < UNITS_PER_N_TILE:
@@ -246,11 +248,11 @@ def tile_binarymlp_pa_kernel(tc, z0, g0, beta0, Wb1, bb1, out):
             quantised = UNITS_PER_N_TILE
             for j in range(N_TILES):
                 for m in range(ROW_TILES):
-                    if m % UNIT_RUN == 0 and binarised < W_UNITS:
+                    if (ROW_TILES * j + m) % UNIT_EVERY == 0 and binarised < W_UNITS:
                         for unit in range(binarised, binarised + UNIT_RUN):
                             binarise(unit, w_psum)
                         binarised += UNIT_RUN
                     out_tile(j, m, acc_psum)
-                    if quantised < binarised:
-                        quantise_w(quantised)
-                        quantised += 1
+                    for unit in range(quantised, min(quantised + 2, binarised)):
+                        quantise_w(unit)
+                    quantised = min(quantised + 2, binarised)

@@ -31,8 +31,7 @@ BN_EPS = 1e-5
 PAIRS = K // (2 * P)
 PSUM_BANKS = 8
 Z_BANKS = 6
-NORM_LAG = 2
-QUANT_LAG = 2
+SUM_SLOTS = 4
 UNIT_RUN = 4
 UNIT_EVERY = 3
 
@@ -53,6 +52,7 @@ def tile_binarymlp_pa_kernel(tc, z0, g0, beta0, Wb1, bb1, out):
         h_stage = ctx.enter_context(tc.tile_pool(name="h_stage", bufs=2))
         w_stage = ctx.enter_context(tc.tile_pool(name="w_stage", bufs=UNIT_RUN))
         o_stage = ctx.enter_context(tc.tile_pool(name="o_stage", bufs=6))
+        junk = ctx.enter_context(tc.tile_pool(name="junk", bufs=2))
 
         ident_bf = const.tile([P, P], BF16)
         make_identity(nc, ident_bf[:])
@@ -60,6 +60,8 @@ def tile_binarymlp_pa_kernel(tc, z0, g0, beta0, Wb1, bb1, out):
         make_identity(nc, ident_f32[:])
         neg_half = const.tile([P, 2], F32)
         nc.gpsimd.memset(neg_half[:], -0.5)
+        ones_bf = const.tile([P, P], BF16)
+        nc.vector.memset(ones_bf[:], 1.0)
 
         vec_rows = const.tile([P, P], F32)
         nc.vector.memset(vec_rows[:], 0.0)
@@ -102,33 +104,58 @@ def tile_binarymlp_pa_kernel(tc, z0, g0, beta0, Wb1, bb1, out):
         w_scales = keep.tile([P, PASSES, N], U8, align_bytes=64)
 
         z_t_of = {}
+        neg_mean_of = {}
+        sq_sum_of = {}
+        h_grouped_of = {}
         scale_of = {}
         offset_of = {}
         h_t_of = {}
         w_grouped_of = {}
+        w_t_of = {}
 
-        def statistics(pair, mean_var, z_psum):
+        def transposes_and_sums(pair, z_psum, sums):
             columns = z_sb[pair][:].rearrange("p r (q e) -> p r e q", e=2)
             for e in range(2):
                 z_t = z_psum.tile([P, BATCH], BF16)
                 for r in range(ROW_TILES):
                     nc.tensor.transpose(z_t[:, r * P : (r + 1) * P], columns[:, r, e, :], ident_bf[:])
                 z_t_of[(pair, e)] = z_t
-            stats = small.tile([P, 2, BATCH // BN_CHUNK, 6], F32)
             for e in range(2):
-                for c in range(BATCH // BN_CHUNK):
-                    nc.vector.bn_stats(
-                        out=stats[:, e, c, :], in_=z_t_of[(pair, e)][:, c * BN_CHUNK : (c + 1) * BN_CHUNK]
+                for r in range(ROW_TILES):
+                    nc.tensor.matmul(
+                        out=sums[:, (2 * pair + e) % SUM_SLOTS, :],
+                        lhsT=columns[:, r, e, :],
+                        rhs=ones_bf[:],
+                        start=(r == 0),
+                        stop=(r == ROW_TILES - 1),
                     )
-            for e in range(2):
-                nc.vector.bn_aggr(out=mean_var[:, e, :], in_=stats[:, e, :, :].rearrange("p c s -> p (c s)"))
 
-        def scale_and_offset(pair, mean_var, gain_shift):
+        def negative_mean(pair, sums):
+            first = (2 * pair) % SUM_SLOTS
+            neg_mean_of[pair] = small.tile([P, 2], F32, name="neg_mean")
+            nc.scalar.activation(
+                out=neg_mean_of[pair][:], in_=sums[:, first : first + 2, 0], func=ACT.Copy, scale=-1.0 / BATCH
+            )
+
+        def squares(pair):
+            sq_sum_of[pair] = small.tile([P, 2], F32, name="sq_sum")
+            for e in range(2):
+                squared = junk.tile([P, BATCH], BF16)
+                nc.scalar.activation(
+                    out=squared[:],
+                    in_=z_t_of[(pair, e)][:],
+                    func=ACT.Square,
+                    bias=neg_mean_of[pair][:, e : e + 1],
+                    scale=1.0,
+                    accum_out=sq_sum_of[pair][:, e : e + 1],
+                )
+
+        def scale_and_offset(pair, gain_shift):
             gain = gain_shift[:, pair : pair + 1].bitcast(BF16)
             shift = gain_shift[:, PAIRS + pair : PAIRS + pair + 1].bitcast(BF16)
             var_eps = small.tile([P, 2], F32)
             nc.gpsimd.tensor_scalar(
-                out=var_eps[:], in0=mean_var[:, :, 1], scalar1=BN_EPS, scalar2=None, op0=ALU.add
+                out=var_eps[:], in0=sq_sum_of[pair][:], scalar1=1.0 / BATCH, scalar2=BN_EPS, op0=ALU.mult, op1=ALU.add
             )
             rstd = small.tile([P, 2], F32)
             nc.gpsimd.tensor_tensor(out=rstd[:], in0=var_eps[:], in1=neg_half[:], op=ALU.pow)
@@ -136,42 +163,47 @@ def tile_binarymlp_pa_kernel(tc, z0, g0, beta0, Wb1, bb1, out):
             nc.gpsimd.tensor_tensor(out=scale_of[pair][:], in0=rstd[:], in1=gain, op=ALU.mult)
             mean_scaled = small.tile([P, 2], F32)
             nc.gpsimd.tensor_tensor(
-                out=mean_scaled[:], in0=mean_var[:, :, 0], in1=scale_of[pair][:], op=ALU.mult
+                out=mean_scaled[:], in0=neg_mean_of[pair][:], in1=scale_of[pair][:], op=ALU.mult
             )
             offset_of[pair] = small.tile([P, 2], F32, name="offset")
-            nc.gpsimd.tensor_tensor(
-                out=offset_of[pair][:], in0=shift, in1=mean_scaled[:], op=ALU.subtract
-            )
+            nc.gpsimd.tensor_tensor(out=offset_of[pair][:], in0=shift, in1=mean_scaled[:], op=ALU.add)
 
-        def norm_relu(pair):
+        def norm(pair):
             g, u = divmod(pair, 2)
             if u == 0:
                 h_t_of[g] = h_stage.tile([P, PACK, BATCH], BF16, name="h_t")
             for e in range(2):
-                nc.scalar.activation(
+                nc.vector.tensor_scalar(
                     out=h_t_of[g][:, 2 * u + e, :],
-                    in_=z_t_of[(pair, e)][:],
-                    func=ACT.Relu,
-                    bias=offset_of[pair][:, e : e + 1],
-                    scale=scale_of[pair][:, e : e + 1],
+                    in0=z_t_of[(pair, e)][:],
+                    scalar1=scale_of[pair][:, e : e + 1],
+                    scalar2=offset_of[pair][:, e : e + 1],
+                    op0=ALU.mult,
+                    op1=ALU.add,
+                )
+
+        halves = [slice(first, first + HALF) for first in range(0, BATCH, HALF)]
+
+        def relu_grouped(g):
+            h_grouped_of[g] = h_stage.tile([P, BATCH, PACK], BF16, align_bytes=64, name="h_grouped")
+            for rows in halves:
+                nc.vector.tensor_scalar(
+                    out=h_grouped_of[g][:, rows, :].rearrange("p (c i) t -> p c t i", i=4),
+                    in0=h_t_of[g][:, :, rows].rearrange("p t (c i) -> p c t i", i=4),
+                    scalar1=0.0,
+                    scalar2=None,
+                    op0=ALU.max,
                 )
 
         def quantise_h(g):
-            h_grouped = h_stage.tile([P, BATCH, PACK], BF16, align_bytes=64)
-            halves = [slice(first, first + HALF) for first in range(0, BATCH, HALF)]
-            for rows in halves:
-                nc.vector.tensor_copy(
-                    out=h_grouped[:, rows, :].rearrange("p (c i) t -> p c t i", i=4),
-                    in_=h_t_of[g][:, :, rows].rearrange("p t (c i) -> p c t i", i=4),
-                )
             for rows in halves:
                 nc.vector.quantize_mx(
                     out=h_codes[:, g, rows].bitcast(FP8X4),
                     scales=h_scales[:, g, rows],
-                    in_=h_grouped[:, rows, :].rearrange("p b t -> p (b t)"),
+                    in_=h_grouped_of[g][:, rows, :].rearrange("p b t -> p (b t)"),
                 )
 
-        def binarise(unit, w_psum):
+        def transposes_w(unit, w_psum):
             c, g = divmod(unit, PASSES)
             words = w_sb[c][:].bitcast(F32)
             w_t = w_psum.tile([P, 2, W_ROWS], F32)
@@ -181,6 +213,10 @@ def tile_binarymlp_pa_kernel(tc, z0, g0, beta0, Wb1, bb1, out):
                     nc.tensor.transpose(
                         w_t[:, u, i * P : (i + 1) * P], words[:, i, first : first + P], ident_f32[:]
                     )
+            w_t_of[unit] = w_t
+
+        def sign_w(unit):
+            w_t = w_t_of[unit]
             w_grouped_of[unit] = w_stage.tile([P, W_ROWS, PACK], BF16, align_bytes=64, name="w_grouped")
             nc.scalar.activation(
                 out=w_grouped_of[unit][:].rearrange("p r (u e) -> p r u e", e=2),
@@ -219,26 +255,34 @@ def tile_binarymlp_pa_kernel(tc, z0, g0, beta0, Wb1, bb1, out):
 
         with ExitStack() as stage:
             z_psum = stage.enter_context(tc.psum_pool(name="z_psum", bufs=Z_BANKS))
-            w_psum = stage.enter_context(tc.psum_pool(name="w_psum_first", bufs=PSUM_BANKS - Z_BANKS))
+            s_psum = stage.enter_context(tc.psum_pool(name="s_psum", bufs=1))
+            w_psum = stage.enter_context(tc.psum_pool(name="w_psum_first", bufs=1))
             gain_shift = const.tile([P, 2 * PAIRS], F32)
-            for step in range(PAIRS + NORM_LAG + QUANT_LAG):
-                if 0 <= step - NORM_LAG < PAIRS:
-                    norm_relu(step - NORM_LAG)
+            sums = s_psum.tile([P, SUM_SLOTS, P], F32)
+            for step in range(PAIRS + 4):
+                if 0 <= step - 1 < PAIRS:
+                    squares(step - 1)
+                    scale_and_offset(step - 1, gain_shift)
                 if step < PAIRS:
-                    mean_var = small.tile([P, 2, 2], F32)
-                    statistics(step, mean_var, z_psum)
+                    transposes_and_sums(step, z_psum, sums)
+                    negative_mean(step, sums)
                     if step == 0:
                         vec_t = w_psum.tile([P, P], F32, tag="w_t")
                         nc.tensor.transpose(vec_t[:], vec_rows[:], ident_f32[:])
                         nc.vector.tensor_copy(out=gain_shift[:], in_=vec_t[:, 0 : 2 * PAIRS])
-                    scale_and_offset(step, mean_var, gain_shift)
-                for unit in range(2 * (step - 1), 2 * step):
-                    if 0 <= unit < UNITS_PER_N_TILE:
-                        binarise(unit, w_psum)
-                    if 0 <= unit - 2 < UNITS_PER_N_TILE:
-                        quantise_w(unit - 2)
-                g, u = divmod(step - NORM_LAG - QUANT_LAG, 2)
-                if g >= 0 and u == 1:
+                unit = step - 1
+                if 0 <= unit < UNITS_PER_N_TILE:
+                    transposes_w(unit, w_psum)
+                    sign_w(unit)
+                if 0 <= step - 2 < PAIRS:
+                    norm(step - 2)
+                if 0 <= unit - 1 < UNITS_PER_N_TILE:
+                    quantise_w(unit - 1)
+                g, u = divmod(step - 2, 2)
+                if 0 <= g < PASSES and u == 1:
+                    relu_grouped(g)
+                g, u = divmod(step - 3, 2)
+                if 0 <= g < PASSES and u == 1:
                     quantise_h(g)
 
         with ExitStack() as stage:
@@ -250,7 +294,8 @@ def tile_binarymlp_pa_kernel(tc, z0, g0, beta0, Wb1, bb1, out):
                 for m in range(ROW_TILES):
                     if (ROW_TILES * j + m) % UNIT_EVERY == 0 and binarised < W_UNITS:
                         for unit in range(binarised, binarised + UNIT_RUN):
-                            binarise(unit, w_psum)
+                            transposes_w(unit, w_psum)
+                            sign_w(unit)
                         binarised += UNIT_RUN
                     out_tile(j, m, acc_psum)
                     for unit in range(quantised, min(quantised + 2, binarised)):

@@ -32,8 +32,15 @@ PAIRS = K // (2 * P)
 PSUM_BANKS = 8
 Z_BANKS = 6
 SUM_SLOTS = 4
+VECTOR_STAT_PAIRS = 2
+SUM_BANK = 6
+UNIT_BANK = 7
+LATE_UNIT_BANKS = (7, 4, 5)
+EARLY_UNIT_STEPS = (4, 6)
+ACC_BANKS = (0, 1, 2, 3)
+W_BANKS = (4, 5, 6, 7)
 UNIT_RUN = 4
-UNIT_EVERY = 3
+UNIT_EVERY = 4
 
 SIGN_SCALE = 2.0**64
 SIGN_BIAS = 2.0**-100
@@ -50,7 +57,8 @@ def tile_binarymlp_pa_kernel(tc, z0, g0, beta0, Wb1, bb1, out):
         keep = ctx.enter_context(tc.tile_pool(name="keep", bufs=1))
         small = ctx.enter_context(tc.tile_pool(name="small", bufs=4))
         h_stage = ctx.enter_context(tc.tile_pool(name="h_stage", bufs=2))
-        w_stage = ctx.enter_context(tc.tile_pool(name="w_stage", bufs=UNIT_RUN))
+        w_stage = ctx.enter_context(tc.tile_pool(name="w_stage", bufs=UNITS_PER_N_TILE))
+        psum = ctx.enter_context(tc.psum_pool(name="psum", bufs=1))
         o_stage = ctx.enter_context(tc.tile_pool(name="o_stage", bufs=6))
         junk = ctx.enter_context(tc.tile_pool(name="junk", bufs=2))
 
@@ -65,13 +73,6 @@ def tile_binarymlp_pa_kernel(tc, z0, g0, beta0, Wb1, bb1, out):
 
         vec_rows = const.tile([P, P], F32)
         nc.vector.memset(vec_rows[:], 0.0)
-        nc.scalar.dma_start(
-            out=vec_rows[0:PAIRS, :].bitcast(BF16), in_=g0.rearrange("(c w) -> c w", c=PAIRS)
-        )
-        nc.scalar.dma_start(
-            out=vec_rows[PAIRS : 2 * PAIRS, :].bitcast(BF16), in_=beta0.rearrange("(c w) -> c w", c=PAIRS)
-        )
-
         z_sb = [inputs.tile([P, ROW_TILES, 2 * P], BF16, name="z_sb%d" % pair) for pair in range(PAIRS)]
         w_sb = [inputs.tile([P, W_ROWS // P, K], BF16, name="w_sb%d" % c) for c in range(W_LOADS)]
 
@@ -87,12 +88,19 @@ def tile_binarymlp_pa_kernel(tc, z0, g0, beta0, Wb1, bb1, out):
                 in_=Wb1[c * W_ROWS : (c + 1) * W_ROWS, :].rearrange("(i p) k -> p i k", p=P),
             )
 
-        for c in range(N_TILE // W_ROWS):
-            load_z(2 * c)
-            load_z(2 * c + 1)
-            load_w(c)
-        for pair in range(2 * (N_TILE // W_ROWS), PAIRS):
+        load_z(0)
+        nc.sync.dma_start(
+            out=vec_rows[0:PAIRS, :].bitcast(BF16), in_=g0.rearrange("(c w) -> c w", c=PAIRS)
+        )
+        nc.sync.dma_start(
+            out=vec_rows[PAIRS : 2 * PAIRS, :].bitcast(BF16), in_=beta0.rearrange("(c w) -> c w", c=PAIRS)
+        )
+        for pair in range(1, 4):
             load_z(pair)
+        for c in range(N_TILE // W_ROWS):
+            load_w(c)
+            load_z(4 + 2 * c)
+            load_z(5 + 2 * c)
         for c in range(N_TILE // W_ROWS, W_LOADS):
             load_w(c)
         bias_bc = const.tile([P, N], BF16)
@@ -113,13 +121,16 @@ def tile_binarymlp_pa_kernel(tc, z0, g0, beta0, Wb1, bb1, out):
         w_grouped_of = {}
         w_t_of = {}
 
-        def transposes_and_sums(pair, z_psum, sums):
+        def transposes_z(pair):
             columns = z_sb[pair][:].rearrange("p r (q e) -> p r e q", e=2)
             for e in range(2):
-                z_t = z_psum.tile([P, BATCH], BF16)
+                z_t = psum.tile([P, BATCH], BF16, tag="bank%d" % ((2 * pair + e) % Z_BANKS))
                 for r in range(ROW_TILES):
                     nc.tensor.transpose(z_t[:, r * P : (r + 1) * P], columns[:, r, e, :], ident_bf[:])
                 z_t_of[(pair, e)] = z_t
+
+        def column_sums(pair, sums):
+            columns = z_sb[pair][:].rearrange("p r (q e) -> p r e q", e=2)
             for e in range(2):
                 for r in range(ROW_TILES):
                     nc.tensor.matmul(
@@ -150,23 +161,33 @@ def tile_binarymlp_pa_kernel(tc, z0, g0, beta0, Wb1, bb1, out):
                     accum_out=sq_sum_of[pair][:, e : e + 1],
                 )
 
-        def scale_and_offset(pair, gain_shift):
+        def vector_statistics(pair):
+            stats = small.tile([P, 2, BATCH // BN_CHUNK, 6], F32)
+            for e in range(2):
+                for c in range(BATCH // BN_CHUNK):
+                    nc.vector.bn_stats(
+                        out=stats[:, e, c, :], in_=z_t_of[(pair, e)][:, c * BN_CHUNK : (c + 1) * BN_CHUNK]
+                    )
+            mean_var = small.tile([P, 2, 2], F32)
+            for e in range(2):
+                nc.vector.bn_aggr(out=mean_var[:, e, :], in_=stats[:, e, :, :].rearrange("p c s -> p (c s)"))
+            return mean_var
+
+        def scale_and_offset(pair, gain_shift, var_like, var_factor, mean_like, mean_op):
             gain = gain_shift[:, pair : pair + 1].bitcast(BF16)
             shift = gain_shift[:, PAIRS + pair : PAIRS + pair + 1].bitcast(BF16)
             var_eps = small.tile([P, 2], F32)
             nc.gpsimd.tensor_scalar(
-                out=var_eps[:], in0=sq_sum_of[pair][:], scalar1=1.0 / BATCH, scalar2=BN_EPS, op0=ALU.mult, op1=ALU.add
+                out=var_eps[:], in0=var_like, scalar1=var_factor, scalar2=BN_EPS, op0=ALU.mult, op1=ALU.add
             )
             rstd = small.tile([P, 2], F32)
             nc.gpsimd.tensor_tensor(out=rstd[:], in0=var_eps[:], in1=neg_half[:], op=ALU.pow)
             scale_of[pair] = small.tile([P, 2], F32, name="scale")
             nc.gpsimd.tensor_tensor(out=scale_of[pair][:], in0=rstd[:], in1=gain, op=ALU.mult)
             mean_scaled = small.tile([P, 2], F32)
-            nc.gpsimd.tensor_tensor(
-                out=mean_scaled[:], in0=neg_mean_of[pair][:], in1=scale_of[pair][:], op=ALU.mult
-            )
+            nc.gpsimd.tensor_tensor(out=mean_scaled[:], in0=mean_like, in1=scale_of[pair][:], op=ALU.mult)
             offset_of[pair] = small.tile([P, 2], F32, name="offset")
-            nc.gpsimd.tensor_tensor(out=offset_of[pair][:], in0=shift, in1=mean_scaled[:], op=ALU.add)
+            nc.gpsimd.tensor_tensor(out=offset_of[pair][:], in0=shift, in1=mean_scaled[:], op=mean_op)
 
         def norm(pair):
             g, u = divmod(pair, 2)
@@ -182,31 +203,27 @@ def tile_binarymlp_pa_kernel(tc, z0, g0, beta0, Wb1, bb1, out):
                     op1=ALU.add,
                 )
 
-        halves = [slice(first, first + HALF) for first in range(0, BATCH, HALF)]
-
         def relu_grouped(g):
             h_grouped_of[g] = h_stage.tile([P, BATCH, PACK], BF16, align_bytes=64, name="h_grouped")
-            for rows in halves:
-                nc.vector.tensor_scalar(
-                    out=h_grouped_of[g][:, rows, :].rearrange("p (c i) t -> p c t i", i=4),
-                    in0=h_t_of[g][:, :, rows].rearrange("p t (c i) -> p c t i", i=4),
-                    scalar1=0.0,
-                    scalar2=None,
-                    op0=ALU.max,
-                )
+            nc.vector.tensor_scalar(
+                out=h_grouped_of[g][:].rearrange("p (c i) t -> p c t i", i=4),
+                in0=h_t_of[g][:].rearrange("p t (c i) -> p c t i", i=4),
+                scalar1=0.0,
+                scalar2=None,
+                op0=ALU.max,
+            )
 
         def quantise_h(g):
-            for rows in halves:
-                nc.vector.quantize_mx(
-                    out=h_codes[:, g, rows].bitcast(FP8X4),
-                    scales=h_scales[:, g, rows],
-                    in_=h_grouped_of[g][:, rows, :].rearrange("p b t -> p (b t)"),
-                )
+            nc.vector.quantize_mx(
+                out=h_codes[:, g, :].bitcast(FP8X4),
+                scales=h_scales[:, g, :],
+                in_=h_grouped_of[g][:].rearrange("p b t -> p (b t)"),
+            )
 
-        def transposes_w(unit, w_psum):
+        def transposes_w(unit, bank):
             c, g = divmod(unit, PASSES)
             words = w_sb[c][:].bitcast(F32)
-            w_t = w_psum.tile([P, 2, W_ROWS], F32)
+            w_t = psum.tile([P, 2, W_ROWS], F32, tag="bank%d" % bank)
             for u in range(2):
                 first = (K_PASS // 2) * g + P * u
                 for i in range(W_ROWS // P):
@@ -235,10 +252,10 @@ def tile_binarymlp_pa_kernel(tc, z0, g0, beta0, Wb1, bb1, out):
                 in_=w_grouped_of[unit][:].rearrange("p r t -> p (r t)"),
             )
 
-        def out_tile(j, m, acc_psum):
+        def out_tile(j, m, bank):
             m_cols = slice(m * P, (m + 1) * P)
             n_cols = slice(j * N_TILE, (j + 1) * N_TILE)
-            acc = acc_psum.tile([P, N_TILE], F32)
+            acc = psum.tile([P, N_TILE], F32, tag="bank%d" % bank)
             for g in range(PASSES):
                 nc.tensor.matmul_mx(
                     out=acc[:],
@@ -253,51 +270,67 @@ def tile_binarymlp_pa_kernel(tc, z0, g0, beta0, Wb1, bb1, out):
             nc.vector.tensor_tensor(out=result[:], in0=acc[:], in1=bias_bc[:, n_cols], op=ALU.add)
             nc.sync.dma_start(out=out[m_cols, n_cols], in_=result[:])
 
-        with ExitStack() as stage:
-            z_psum = stage.enter_context(tc.psum_pool(name="z_psum", bufs=Z_BANKS))
-            s_psum = stage.enter_context(tc.psum_pool(name="s_psum", bufs=1))
-            w_psum = stage.enter_context(tc.psum_pool(name="w_psum_first", bufs=1))
-            gain_shift = const.tile([P, 2 * PAIRS], F32)
-            sums = s_psum.tile([P, SUM_SLOTS, P], F32)
-            for step in range(PAIRS + 4):
-                if 0 <= step - 1 < PAIRS:
-                    squares(step - 1)
-                    scale_and_offset(step - 1, gain_shift)
-                if step < PAIRS:
-                    transposes_and_sums(step, z_psum, sums)
-                    negative_mean(step, sums)
+        gain_shift = const.tile([P, 2 * PAIRS], F32)
+        sums = psum.tile([P, SUM_SLOTS, P], F32, tag="bank%d" % SUM_BANK)
+        first_units = [PASSES * c + g for g in range(PASSES) for c in range(N_TILE // W_ROWS)]
+        signed = []
+        for step in range(PAIRS + 2):
+            if VECTOR_STAT_PAIRS <= step - 1 < PAIRS:
+                squares(step - 1)
+                scale_and_offset(
+                    step - 1, gain_shift, sq_sum_of[step - 1][:], 1.0 / BATCH, neg_mean_of[step - 1][:], ALU.add
+                )
+            if step < PAIRS:
+                transposes_z(step)
+                if step == 0:
+                    vec_t = psum.tile([P, P], F32, tag="bank%d" % UNIT_BANK)
+                    nc.tensor.transpose(vec_t[:], vec_rows[:], ident_f32[:])
+                if step < VECTOR_STAT_PAIRS:
+                    mean_var = vector_statistics(step)
                     if step == 0:
-                        vec_t = w_psum.tile([P, P], F32, tag="w_t")
-                        nc.tensor.transpose(vec_t[:], vec_rows[:], ident_f32[:])
                         nc.vector.tensor_copy(out=gain_shift[:], in_=vec_t[:, 0 : 2 * PAIRS])
-                unit = step - 1
-                if 0 <= unit < UNITS_PER_N_TILE:
-                    transposes_w(unit, w_psum)
+                    scale_and_offset(step, gain_shift, mean_var[:, :, 1], 1.0, mean_var[:, :, 0], ALU.subtract)
+                else:
+                    column_sums(step, sums)
+                    negative_mean(step, sums)
+            if step in EARLY_UNIT_STEPS:
+                unit = first_units[len(signed)]
+                transposes_w(unit, UNIT_BANK)
+                sign_w(unit)
+                signed.append(unit)
+            if step == PAIRS:
+                for unit in first_units[len(signed) :]:
+                    transposes_w(unit, LATE_UNIT_BANKS[len(signed) % len(LATE_UNIT_BANKS)])
                     sign_w(unit)
-                if 0 <= step - 2 < PAIRS:
-                    norm(step - 2)
-                if 0 <= unit - 1 < UNITS_PER_N_TILE:
-                    quantise_w(unit - 1)
-                g, u = divmod(step - 2, 2)
-                if 0 <= g < PASSES and u == 1:
-                    relu_grouped(g)
-                g, u = divmod(step - 3, 2)
-                if 0 <= g < PASSES and u == 1:
-                    quantise_h(g)
+                    signed.append(unit)
+            if 0 <= step - 2 < PAIRS:
+                norm(step - 2)
+            g, u = divmod(step - 2, 2)
+            if 0 <= g < PASSES - 1 and u == 1:
+                relu_grouped(g)
+            g, u = divmod(step - 3, 2)
+            if 0 <= g < PASSES - 1 and u == 1:
+                quantise_h(g)
+        for unit in signed[0:2]:
+            quantise_w(unit)
+        relu_grouped(PASSES - 1)
+        for unit in signed[2:4]:
+            quantise_w(unit)
+        quantise_h(PASSES - 1)
+        for unit in signed[4:]:
+            quantise_w(unit)
 
-        with ExitStack() as stage:
-            acc_psum = stage.enter_context(tc.psum_pool(name="acc_psum", bufs=4, reuse_waits="tile"))
-            w_psum = stage.enter_context(tc.psum_pool(name="w_psum_second", bufs=UNIT_RUN, reuse_waits="tile"))
-            binarised = UNITS_PER_N_TILE
-            quantised = UNITS_PER_N_TILE
-            for j in range(N_TILES):
-                for m in range(ROW_TILES):
-                    if (ROW_TILES * j + m) % UNIT_EVERY == 0 and binarised < W_UNITS:
-                        for unit in range(binarised, binarised + UNIT_RUN):
-                            transposes_w(unit, w_psum)
-                            sign_w(unit)
-                        binarised += UNIT_RUN
-                    out_tile(j, m, acc_psum)
-                    for unit in range(quantised, min(quantised + 2, binarised)):
-                        quantise_w(unit)
-                    quantised = min(quantised + 2, binarised)
+        binarised = UNITS_PER_N_TILE
+        quantised = UNITS_PER_N_TILE
+        for j in range(N_TILES):
+            for m in range(ROW_TILES):
+                tile_index = ROW_TILES * j + m
+                if tile_index % UNIT_EVERY == 0 and binarised < W_UNITS:
+                    for unit in range(binarised, binarised + UNIT_RUN):
+                        transposes_w(unit, W_BANKS[unit % len(W_BANKS)])
+                        sign_w(unit)
+                    binarised += UNIT_RUN
+                out_tile(j, m, ACC_BANKS[tile_index % len(ACC_BANKS)])
+                for unit in range(quantised, min(quantised + 2, binarised)):
+                    quantise_w(unit)
+                quantised = min(quantised + 2, binarised)

@@ -70,6 +70,10 @@ def tile_binarymlp_pa_kernel(tc, z0, g0, beta0, Wb1, bb1, out):
         nc.gpsimd.memset(neg_half[:], -0.5)
         ones_bf = const.tile([P, P], BF16)
         nc.vector.memset(ones_bf[:], 1.0)
+        gain_mean = const.tile([P, PAIRS, 2, 2], F32)
+        zero_shift = const.tile([P, PAIRS, 2, 2], F32)
+        nc.gpsimd.memset(zero_shift[:], 0.0)
+        neg_gain = const.tile([P, PAIRS, 2], F32)
 
         vec_rows = const.tile([P, P], F32)
         nc.vector.memset(vec_rows[:], 0.0)
@@ -115,8 +119,8 @@ def tile_binarymlp_pa_kernel(tc, z0, g0, beta0, Wb1, bb1, out):
         neg_mean_of = {}
         sq_sum_of = {}
         h_grouped_of = {}
-        scale_of = {}
-        offset_of = {}
+        rstd_of = {}
+        scale_offset_of = {}
         h_t_of = {}
         w_grouped_of = {}
         w_t_of = {}
@@ -173,21 +177,28 @@ def tile_binarymlp_pa_kernel(tc, z0, g0, beta0, Wb1, bb1, out):
                 nc.vector.bn_aggr(out=mean_var[:, e, :], in_=stats[:, e, :, :].rearrange("p c s -> p (c s)"))
             return mean_var
 
-        def scale_and_offset(pair, gain_shift, var_like, var_factor, mean_like, mean_op):
-            gain = gain_shift[:, pair : pair + 1].bitcast(BF16)
-            shift = gain_shift[:, PAIRS + pair : PAIRS + pair + 1].bitcast(BF16)
+        def mean_times_gain(pair, mean_like, gain_like):
+            nc.gpsimd.tensor_tensor(out=gain_mean[:, pair, :, 1], in0=mean_like, in1=gain_like, op=ALU.mult)
+
+        def inverse_std(pair, var_like, var_factor):
             var_eps = small.tile([P, 2], F32)
             nc.gpsimd.tensor_scalar(
                 out=var_eps[:], in0=var_like, scalar1=var_factor, scalar2=BN_EPS, op0=ALU.mult, op1=ALU.add
             )
-            rstd = small.tile([P, 2], F32)
-            nc.gpsimd.tensor_tensor(out=rstd[:], in0=var_eps[:], in1=neg_half[:], op=ALU.pow)
-            scale_of[pair] = small.tile([P, 2], F32, name="scale")
-            nc.gpsimd.tensor_tensor(out=scale_of[pair][:], in0=rstd[:], in1=gain, op=ALU.mult)
-            mean_scaled = small.tile([P, 2], F32)
-            nc.gpsimd.tensor_tensor(out=mean_scaled[:], in0=mean_like, in1=scale_of[pair][:], op=ALU.mult)
-            offset_of[pair] = small.tile([P, 2], F32, name="offset")
-            nc.gpsimd.tensor_tensor(out=offset_of[pair][:], in0=shift, in1=mean_scaled[:], op=mean_op)
+            rstd_of[pair] = small.tile([P, 2], F32, name="rstd")
+            nc.gpsimd.tensor_tensor(out=rstd_of[pair][:], in0=var_eps[:], in1=neg_half[:], op=ALU.pow)
+
+        def scale_and_offset(pair):
+            scale_offset_of[pair] = small.tile([P, 2, 2], F32, name="scale_offset")
+            for e in range(2):
+                nc.vector.scalar_tensor_tensor(
+                    out=scale_offset_of[pair][:, e, :],
+                    in0=gain_mean[:, pair, e, :],
+                    scalar=rstd_of[pair][:, e : e + 1],
+                    in1=zero_shift[:, pair, e, :],
+                    op0=ALU.mult,
+                    op1=ALU.add,
+                )
 
         def norm(pair):
             g, u = divmod(pair, 2)
@@ -197,8 +208,8 @@ def tile_binarymlp_pa_kernel(tc, z0, g0, beta0, Wb1, bb1, out):
                 nc.vector.tensor_scalar(
                     out=h_t_of[g][:, 2 * u + e, :],
                     in0=z_t_of[(pair, e)][:],
-                    scalar1=scale_of[pair][:, e : e + 1],
-                    scalar2=offset_of[pair][:, e : e + 1],
+                    scalar1=scale_offset_of[pair][:, e, 0:1],
+                    scalar2=scale_offset_of[pair][:, e, 1:2],
                     op0=ALU.mult,
                     op1=ALU.add,
                 )
@@ -277,22 +288,28 @@ def tile_binarymlp_pa_kernel(tc, z0, g0, beta0, Wb1, bb1, out):
         for step in range(PAIRS + 2):
             if VECTOR_STAT_PAIRS <= step - 1 < PAIRS:
                 squares(step - 1)
-                scale_and_offset(
-                    step - 1, gain_shift, sq_sum_of[step - 1][:], 1.0 / BATCH, neg_mean_of[step - 1][:], ALU.add
-                )
+                inverse_std(step - 1, sq_sum_of[step - 1][:], 1.0 / BATCH)
             if step < PAIRS:
                 transposes_z(step)
                 if step == 0:
                     vec_t = psum.tile([P, P], F32, tag="bank%d" % UNIT_BANK)
                     nc.tensor.transpose(vec_t[:], vec_rows[:], ident_f32[:])
+                    nc.vector.tensor_copy(out=gain_shift[:], in_=vec_t[:, 0 : 2 * PAIRS])
+                    gain = gain_shift[:, 0:PAIRS].bitcast(BF16).rearrange("p (c e) -> p c e", e=2)
+                    shift = gain_shift[:, PAIRS : 2 * PAIRS].bitcast(BF16).rearrange("p (c e) -> p c e", e=2)
+                    nc.gpsimd.tensor_copy(out=gain_mean[:, :, :, 0], in_=gain)
+                    nc.gpsimd.tensor_scalar(
+                        out=neg_gain[:], in0=gain, scalar1=-1.0, scalar2=0.0, op0=ALU.mult, op1=ALU.add
+                    )
+                    nc.gpsimd.tensor_copy(out=zero_shift[:, :, :, 1], in_=shift)
                 if step < VECTOR_STAT_PAIRS:
                     mean_var = vector_statistics(step)
-                    if step == 0:
-                        nc.vector.tensor_copy(out=gain_shift[:], in_=vec_t[:, 0 : 2 * PAIRS])
-                    scale_and_offset(step, gain_shift, mean_var[:, :, 1], 1.0, mean_var[:, :, 0], ALU.subtract)
+                    mean_times_gain(step, mean_var[:, :, 0], neg_gain[:, step, :])
+                    inverse_std(step, mean_var[:, :, 1], 1.0)
                 else:
                     column_sums(step, sums)
                     negative_mean(step, sums)
+                    mean_times_gain(step, neg_mean_of[step][:], gain_mean[:, step, :, 0])
             if step in EARLY_UNIT_STEPS:
                 unit = first_units[len(signed)]
                 transposes_w(unit, UNIT_BANK)
@@ -304,6 +321,7 @@ def tile_binarymlp_pa_kernel(tc, z0, g0, beta0, Wb1, bb1, out):
                     sign_w(unit)
                     signed.append(unit)
             if 0 <= step - 2 < PAIRS:
+                scale_and_offset(step - 2)
                 norm(step - 2)
             g, u = divmod(step - 2, 2)
             if 0 <= g < PASSES - 1 and u == 1:

@@ -66,8 +66,6 @@ def tile_binarymlp_pa_kernel(tc, z0, g0, beta0, Wb1, bb1, out):
         make_identity(nc, ident_bf[:])
         ident_f32 = const.tile([P, P], F32)
         make_identity(nc, ident_f32[:])
-        neg_half = const.tile([P, 2], F32)
-        nc.gpsimd.memset(neg_half[:], -0.5)
         ones_bf = const.tile([P, P], BF16)
         nc.vector.memset(ones_bf[:], 1.0)
         gain_mean = const.tile([P, PAIRS, 2, 2], F32)
@@ -120,6 +118,8 @@ def tile_binarymlp_pa_kernel(tc, z0, g0, beta0, Wb1, bb1, out):
         sq_sum_of = {}
         h_grouped_of = {}
         rstd_of = {}
+        std_of = {}
+        mean_var_of = {}
         scale_offset_of = {}
         h_t_of = {}
         w_grouped_of = {}
@@ -181,12 +181,12 @@ def tile_binarymlp_pa_kernel(tc, z0, g0, beta0, Wb1, bb1, out):
             nc.gpsimd.tensor_tensor(out=gain_mean[:, pair, :, 1], in0=mean_like, in1=gain_like, op=ALU.mult)
 
         def inverse_std(pair, var_like, var_factor):
-            var_eps = small.tile([P, 2], F32)
-            nc.gpsimd.tensor_scalar(
-                out=var_eps[:], in0=var_like, scalar1=var_factor, scalar2=BN_EPS, op0=ALU.mult, op1=ALU.add
-            )
+            std_of[pair] = small.tile([P, 2], F32, name="std")
+            nc.scalar.activation(out=std_of[pair][:], in_=var_like, func=ACT.Sqrt, bias=BN_EPS, scale=var_factor)
+
+        def reciprocal_std(pair):
             rstd_of[pair] = small.tile([P, 2], F32, name="rstd")
-            nc.gpsimd.tensor_tensor(out=rstd_of[pair][:], in0=var_eps[:], in1=neg_half[:], op=ALU.pow)
+            nc.vector.reciprocal(out=rstd_of[pair][:], in_=std_of[pair][:])
 
         def scale_and_offset(pair):
             scale_offset_of[pair] = small.tile([P, 2, 2], F32, name="scale_offset")
@@ -286,30 +286,31 @@ def tile_binarymlp_pa_kernel(tc, z0, g0, beta0, Wb1, bb1, out):
         first_units = [PASSES * c + g for g in range(PASSES) for c in range(N_TILE // W_ROWS)]
         signed = []
         for step in range(PAIRS + 2):
-            if VECTOR_STAT_PAIRS <= step - 1 < PAIRS:
-                squares(step - 1)
-                inverse_std(step - 1, sq_sum_of[step - 1][:], 1.0 / BATCH)
             if step < PAIRS:
                 transposes_z(step)
-                if step == 0:
-                    vec_t = psum.tile([P, P], F32, tag="bank%d" % UNIT_BANK)
-                    nc.tensor.transpose(vec_t[:], vec_rows[:], ident_f32[:])
-                    nc.vector.tensor_copy(out=gain_shift[:], in_=vec_t[:, 0 : 2 * PAIRS])
-                    gain = gain_shift[:, 0:PAIRS].bitcast(BF16).rearrange("p (c e) -> p c e", e=2)
-                    shift = gain_shift[:, PAIRS : 2 * PAIRS].bitcast(BF16).rearrange("p (c e) -> p c e", e=2)
-                    nc.gpsimd.tensor_copy(out=gain_mean[:, :, :, 0], in_=gain)
-                    nc.gpsimd.tensor_scalar(
-                        out=neg_gain[:], in0=gain, scalar1=-1.0, scalar2=0.0, op0=ALU.mult, op1=ALU.add
-                    )
-                    nc.gpsimd.tensor_copy(out=zero_shift[:, :, :, 1], in_=shift)
-                if step < VECTOR_STAT_PAIRS:
-                    mean_var = vector_statistics(step)
-                    mean_times_gain(step, mean_var[:, :, 0], neg_gain[:, step, :])
-                    inverse_std(step, mean_var[:, :, 1], 1.0)
-                else:
-                    column_sums(step, sums)
-                    negative_mean(step, sums)
-                    mean_times_gain(step, neg_mean_of[step][:], gain_mean[:, step, :, 0])
+            if step == 0:
+                vec_t = psum.tile([P, P], F32, tag="bank%d" % UNIT_BANK)
+                nc.tensor.transpose(vec_t[:], vec_rows[:], ident_f32[:])
+                nc.vector.tensor_copy(out=gain_shift[:], in_=vec_t[:, 0 : 2 * PAIRS])
+                gain = gain_shift[:, 0:PAIRS].bitcast(BF16).rearrange("p (c e) -> p c e", e=2)
+                shift = gain_shift[:, PAIRS : 2 * PAIRS].bitcast(BF16).rearrange("p (c e) -> p c e", e=2)
+                nc.gpsimd.tensor_copy(out=gain_mean[:, :, :, 0], in_=gain)
+                nc.gpsimd.tensor_scalar(
+                    out=neg_gain[:], in0=gain, scalar1=-1.0, scalar2=0.0, op0=ALU.mult, op1=ALU.add
+                )
+                nc.gpsimd.tensor_copy(out=zero_shift[:, :, :, 1], in_=shift)
+            if step < VECTOR_STAT_PAIRS:
+                mean_var_of[step] = vector_statistics(step)
+                mean_times_gain(step, mean_var_of[step][:, :, 0], neg_gain[:, step, :])
+            elif step < PAIRS:
+                squares(step)
+                inverse_std(step, sq_sum_of[step][:], 1.0 / BATCH)
+            if 0 <= step - 1 < VECTOR_STAT_PAIRS:
+                inverse_std(step - 1, mean_var_of[step - 1][:, :, 1], 1.0)
+            if VECTOR_STAT_PAIRS <= step + 1 < PAIRS:
+                column_sums(step + 1, sums)
+                negative_mean(step + 1, sums)
+                mean_times_gain(step + 1, neg_mean_of[step + 1][:], gain_mean[:, step + 1, :, 0])
             if step in EARLY_UNIT_STEPS:
                 unit = first_units[len(signed)]
                 transposes_w(unit, UNIT_BANK)
@@ -323,6 +324,8 @@ def tile_binarymlp_pa_kernel(tc, z0, g0, beta0, Wb1, bb1, out):
             if 0 <= step - 2 < PAIRS:
                 scale_and_offset(step - 2)
                 norm(step - 2)
+            if 0 <= step - 1 < PAIRS:
+                reciprocal_std(step - 1)
             g, u = divmod(step - 2, 2)
             if 0 <= g < PASSES - 1 and u == 1:
                 relu_grouped(g)

@@ -35,7 +35,8 @@ SUM_SLOTS = 4
 VECTOR_STAT_PAIRS = 2
 SUM_BANK = 6
 UNIT_BANK = 7
-LATE_UNIT_BANKS = (7, 4, 5)
+LATE_UNIT_BANKS = (7, 4, 5, 6)
+OPEN_TILES = 4
 EARLY_UNIT_STEPS = (4, 6)
 ACC_BANKS = (0, 1, 2, 3)
 W_BANKS = (4, 5, 6, 7)
@@ -57,7 +58,7 @@ def tile_binarymlp_pa_kernel(tc, z0, g0, beta0, Wb1, bb1, out):
         keep = ctx.enter_context(tc.tile_pool(name="keep", bufs=1))
         small = ctx.enter_context(tc.tile_pool(name="small", bufs=4))
         h_stage = ctx.enter_context(tc.tile_pool(name="h_stage", bufs=2))
-        w_stage = ctx.enter_context(tc.tile_pool(name="w_stage", bufs=UNITS_PER_N_TILE))
+        w_stage = ctx.enter_context(tc.tile_pool(name="w_stage", bufs=PASSES))
         psum = ctx.enter_context(tc.psum_pool(name="psum", bufs=1))
         o_stage = ctx.enter_context(tc.tile_pool(name="o_stage", bufs=6))
         junk = ctx.enter_context(tc.tile_pool(name="junk", bufs=2))
@@ -124,6 +125,7 @@ def tile_binarymlp_pa_kernel(tc, z0, g0, beta0, Wb1, bb1, out):
         h_t_of = {}
         w_grouped_of = {}
         w_t_of = {}
+        acc_of = {}
 
         def transposes_z(pair):
             columns = z_sb[pair][:].rearrange("p r (q e) -> p r e q", e=2)
@@ -245,45 +247,60 @@ def tile_binarymlp_pa_kernel(tc, z0, g0, beta0, Wb1, bb1, out):
 
         def sign_w(unit):
             w_t = w_t_of[unit]
-            w_grouped_of[unit] = w_stage.tile([P, W_ROWS, PACK], BF16, align_bytes=64, name="w_grouped")
+            c, g = divmod(unit, PASSES)
+            j, half = divmod(c, N_TILE // W_ROWS)
+            if half == 0:
+                w_grouped_of[(j, g)] = w_stage.tile([P, N_TILE, PACK], BF16, align_bytes=64, name="w_grouped")
             nc.scalar.activation(
-                out=w_grouped_of[unit][:].rearrange("p r (u e) -> p r u e", e=2),
+                out=w_grouped_of[(j, g)][:, half * W_ROWS : (half + 1) * W_ROWS, :].rearrange(
+                    "p r (u e) -> p r u e", e=2
+                ),
                 in_=w_t[:].bitcast(BF16).rearrange("p u (r e) -> p r u e", e=2),
                 func=ACT.Sign,
                 bias=SIGN_BIAS,
                 scale=SIGN_SCALE,
             )
 
-        def quantise_w(unit):
-            c, g = divmod(unit, PASSES)
-            n_cols = slice(c * W_ROWS, (c + 1) * W_ROWS)
+        def quantise_w(j, g):
+            n_cols = slice(j * N_TILE, (j + 1) * N_TILE)
             nc.vector.quantize_mx(
                 out=w_codes[:, g, n_cols].bitcast(FP8X4),
                 scales=w_scales[:, g, n_cols],
-                in_=w_grouped_of[unit][:].rearrange("p r t -> p (r t)"),
+                in_=w_grouped_of[(j, g)][:].rearrange("p r t -> p (r t)"),
             )
 
-        def out_tile(j, m, bank):
+        def one_pass(j, m, g):
+            if g == 0:
+                acc = psum.tile([P, N_TILE], F32, tag="bank%d" % ACC_BANKS[m % len(ACC_BANKS)])
+                acc_of[(j, m)] = acc
             m_cols = slice(m * P, (m + 1) * P)
             n_cols = slice(j * N_TILE, (j + 1) * N_TILE)
-            acc = psum.tile([P, N_TILE], F32, tag="bank%d" % bank)
-            for g in range(PASSES):
-                nc.tensor.matmul_mx(
-                    out=acc[:],
-                    lhsT=h_codes[:, g, m_cols].bitcast(FP8X4),
-                    lhsT_scale=h_scales[:, g, m_cols],
-                    rhs=w_codes[:, g, n_cols].bitcast(FP8X4),
-                    rhs_scale=w_scales[:, g, n_cols],
-                    start=(g == 0),
-                    stop=(g == PASSES - 1),
-                )
+            nc.tensor.matmul_mx(
+                out=acc_of[(j, m)][:],
+                lhsT=h_codes[:, g, m_cols].bitcast(FP8X4),
+                lhsT_scale=h_scales[:, g, m_cols],
+                rhs=w_codes[:, g, n_cols].bitcast(FP8X4),
+                rhs_scale=w_scales[:, g, n_cols],
+                start=(g == 0),
+                stop=(g == PASSES - 1),
+            )
+
+        def bias_and_store(j, m):
+            m_cols = slice(m * P, (m + 1) * P)
+            n_cols = slice(j * N_TILE, (j + 1) * N_TILE)
             result = o_stage.tile([P, N_TILE], F32)
-            nc.vector.tensor_tensor(out=result[:], in0=acc[:], in1=bias_bc[:, n_cols], op=ALU.add)
+            nc.vector.tensor_tensor(out=result[:], in0=acc_of[(j, m)][:], in1=bias_bc[:, n_cols], op=ALU.add)
             nc.sync.dma_start(out=out[m_cols, n_cols], in_=result[:])
 
         gain_shift = const.tile([P, 2 * PAIRS], F32)
         sums = psum.tile([P, SUM_SLOTS, P], F32, tag="bank%d" % SUM_BANK)
-        first_units = [PASSES * c + g for g in range(PASSES) for c in range(N_TILE // W_ROWS)]
+        unit_order = [
+            PASSES * ((N_TILE // W_ROWS) * j + half) + g
+            for j in range(N_TILES)
+            for g in range(PASSES)
+            for half in range(N_TILE // W_ROWS)
+        ]
+        first_units = unit_order[0:UNITS_PER_N_TILE]
         signed = []
         for step in range(PAIRS + 2):
             if step < PAIRS:
@@ -317,8 +334,8 @@ def tile_binarymlp_pa_kernel(tc, z0, g0, beta0, Wb1, bb1, out):
                 sign_w(unit)
                 signed.append(unit)
             if step == PAIRS:
-                for unit in first_units[len(signed) :]:
-                    transposes_w(unit, LATE_UNIT_BANKS[len(signed) % len(LATE_UNIT_BANKS)])
+                for unit in unit_order[len(signed) : UNITS_PER_N_TILE + UNIT_RUN]:
+                    transposes_w(unit, LATE_UNIT_BANKS[(len(signed) - len(EARLY_UNIT_STEPS)) % len(LATE_UNIT_BANKS)])
                     sign_w(unit)
                     signed.append(unit)
             if 0 <= step - 2 < PAIRS:
@@ -332,26 +349,46 @@ def tile_binarymlp_pa_kernel(tc, z0, g0, beta0, Wb1, bb1, out):
             g, u = divmod(step - 3, 2)
             if 0 <= g < PASSES - 1 and u == 1:
                 quantise_h(g)
-        for unit in signed[0:2]:
-            quantise_w(unit)
+        quantise_w(0, 0)
+        for m in range(OPEN_TILES):
+            one_pass(0, m, 0)
         relu_grouped(PASSES - 1)
-        for unit in signed[2:4]:
-            quantise_w(unit)
+        quantise_w(0, 1)
+        for m in range(OPEN_TILES):
+            one_pass(0, m, 1)
         quantise_h(PASSES - 1)
-        for unit in signed[4:]:
-            quantise_w(unit)
+        quantise_w(0, 2)
+        for m in range(OPEN_TILES):
+            one_pass(0, m, 2)
+        quantise_w(0, 3)
+        for m in range(OPEN_TILES):
+            one_pass(0, m, 3)
 
-        binarised = UNITS_PER_N_TILE
+        binarised = len(signed)
         quantised = UNITS_PER_N_TILE
+
+        def run_of_units(first):
+            for position in range(first, min(first + UNIT_RUN, W_UNITS)):
+                transposes_w(unit_order[position], LATE_UNIT_BANKS[(position - len(EARLY_UNIT_STEPS)) % len(LATE_UNIT_BANKS)])
+                sign_w(unit_order[position])
+            return min(first + UNIT_RUN, W_UNITS)
+
         for j in range(N_TILES):
-            for m in range(ROW_TILES):
-                tile_index = ROW_TILES * j + m
-                if tile_index % UNIT_EVERY == 0 and binarised < W_UNITS:
-                    for unit in range(binarised, binarised + UNIT_RUN):
-                        transposes_w(unit, W_BANKS[unit % len(W_BANKS)])
-                        sign_w(unit)
-                    binarised += UNIT_RUN
-                out_tile(j, m, ACC_BANKS[tile_index % len(ACC_BANKS)])
-                for unit in range(quantised, min(quantised + 2, binarised)):
-                    quantise_w(unit)
-                quantised = min(quantised + 2, binarised)
+            if j > 0:
+                binarised = run_of_units(binarised)
+                for g in range(PASSES):
+                    for m in range(OPEN_TILES):
+                        one_pass(j, m, g)
+            for m in range(OPEN_TILES):
+                bias_and_store(j, m)
+                if quantised < binarised:
+                    quantise_w(quantised // UNITS_PER_N_TILE, (quantised % UNITS_PER_N_TILE) // 2)
+                    quantised += 2
+            binarised = run_of_units(binarised)
+            for m in range(OPEN_TILES, ROW_TILES):
+                for g in range(PASSES):
+                    one_pass(j, m, g)
+                bias_and_store(j, m)
+                if quantised < binarised:
+                    quantise_w(quantised // UNITS_PER_N_TILE, (quantised % UNITS_PER_N_TILE) // 2)
+                    quantised += 2

@@ -167,13 +167,15 @@ def tile_binarymlp_pa_kernel(tc, z0, g0, beta0, Wb1, bb1, out):
                     accum_out=sq_sum_of[pair][:, e : e + 1],
                 )
 
-        def vector_statistics(pair):
+        def vector_statistics(pair, between):
             stats = small.tile([P, 2, BATCH // BN_CHUNK, 6], F32)
             for e in range(2):
                 for c in range(BATCH // BN_CHUNK):
                     nc.vector.bn_stats(
                         out=stats[:, e, c, :], in_=z_t_of[(pair, e)][:, c * BN_CHUNK : (c + 1) * BN_CHUNK]
                     )
+                if e == 0:
+                    between()
             mean_var = small.tile([P, 2, 2], F32)
             for e in range(2):
                 nc.vector.bn_aggr(out=mean_var[:, e, :], in_=stats[:, e, :, :].rearrange("p c s -> p (c s)"))
@@ -269,14 +271,14 @@ def tile_binarymlp_pa_kernel(tc, z0, g0, beta0, Wb1, bb1, out):
                 in_=w_grouped_of[(j, g)][:].rearrange("p r t -> p (r t)"),
             )
 
-        def one_pass(j, m, g):
+        def one_pass(j, m, g, first=0, width=N_TILE):
             if g == 0:
-                acc = psum.tile([P, N_TILE], F32, tag="bank%d" % ACC_BANKS[m % len(ACC_BANKS)])
-                acc_of[(j, m)] = acc
+                acc = psum.tile([P, width], F32, tag="bank%d" % ACC_BANKS[(m + first // width) % len(ACC_BANKS)])
+                acc_of[(j, m, first)] = acc
             m_cols = slice(m * P, (m + 1) * P)
-            n_cols = slice(j * N_TILE, (j + 1) * N_TILE)
+            n_cols = slice(j * N_TILE + first, j * N_TILE + first + width)
             nc.tensor.matmul_mx(
-                out=acc_of[(j, m)][:],
+                out=acc_of[(j, m, first)][:],
                 lhsT=h_codes[:, g, m_cols].bitcast(FP8X4),
                 lhsT_scale=h_scales[:, g, m_cols],
                 rhs=w_codes[:, g, n_cols].bitcast(FP8X4),
@@ -285,12 +287,14 @@ def tile_binarymlp_pa_kernel(tc, z0, g0, beta0, Wb1, bb1, out):
                 stop=(g == PASSES - 1),
             )
 
-        def bias_and_store(j, m):
+        def bias_and_store(j, m, first=0, width=N_TILE):
             m_cols = slice(m * P, (m + 1) * P)
-            n_cols = slice(j * N_TILE, (j + 1) * N_TILE)
+            n_cols = slice(j * N_TILE + first, j * N_TILE + first + width)
             result = o_stage.tile([P, N_TILE], F32)
-            nc.vector.tensor_tensor(out=result[:], in0=acc_of[(j, m)][:], in1=bias_bc[:, n_cols], op=ALU.add)
-            nc.sync.dma_start(out=out[m_cols, n_cols], in_=result[:])
+            nc.vector.tensor_tensor(
+                out=result[:, 0:width], in0=acc_of[(j, m, first)][:], in1=bias_bc[:, n_cols], op=ALU.add
+            )
+            nc.sync.dma_start(out=out[m_cols, n_cols], in_=result[:, 0:width])
 
         gain_shift = const.tile([P, 2 * PAIRS], F32)
         sums = psum.tile([P, SUM_SLOTS, P], F32, tag="bank%d" % SUM_BANK)
@@ -302,22 +306,26 @@ def tile_binarymlp_pa_kernel(tc, z0, g0, beta0, Wb1, bb1, out):
         ]
         first_units = unit_order[0:UNITS_PER_N_TILE]
         signed = []
+        vec_t = psum.tile([P, P], F32, tag="bank%d" % UNIT_BANK)
+
+        def spread_gain_and_shift():
+            nc.vector.tensor_copy(out=gain_shift[:], in_=vec_t[:, 0 : 2 * PAIRS])
+            gain = gain_shift[:, 0:PAIRS].bitcast(BF16).rearrange("p (c e) -> p c e", e=2)
+            shift = gain_shift[:, PAIRS : 2 * PAIRS].bitcast(BF16).rearrange("p (c e) -> p c e", e=2)
+            nc.gpsimd.tensor_copy(out=gain_mean[:, :, :, 0], in_=gain)
+            nc.gpsimd.tensor_scalar(out=neg_gain[:], in0=gain, scalar1=-1.0, scalar2=0.0, op0=ALU.mult, op1=ALU.add)
+            nc.gpsimd.tensor_copy(out=zero_shift[:, :, :, 1], in_=shift)
+
+        def nothing():
+            return None
+
         for step in range(PAIRS + 2):
             if step < PAIRS:
                 transposes_z(step)
             if step == 0:
-                vec_t = psum.tile([P, P], F32, tag="bank%d" % UNIT_BANK)
                 nc.tensor.transpose(vec_t[:], vec_rows[:], ident_f32[:])
-                nc.vector.tensor_copy(out=gain_shift[:], in_=vec_t[:, 0 : 2 * PAIRS])
-                gain = gain_shift[:, 0:PAIRS].bitcast(BF16).rearrange("p (c e) -> p c e", e=2)
-                shift = gain_shift[:, PAIRS : 2 * PAIRS].bitcast(BF16).rearrange("p (c e) -> p c e", e=2)
-                nc.gpsimd.tensor_copy(out=gain_mean[:, :, :, 0], in_=gain)
-                nc.gpsimd.tensor_scalar(
-                    out=neg_gain[:], in0=gain, scalar1=-1.0, scalar2=0.0, op0=ALU.mult, op1=ALU.add
-                )
-                nc.gpsimd.tensor_copy(out=zero_shift[:, :, :, 1], in_=shift)
             if step < VECTOR_STAT_PAIRS:
-                mean_var_of[step] = vector_statistics(step)
+                mean_var_of[step] = vector_statistics(step, spread_gain_and_shift if step == 0 else nothing)
                 mean_times_gain(step, mean_var_of[step][:, :, 0], neg_gain[:, step, :])
             elif step < PAIRS:
                 squares(step)
@@ -386,9 +394,11 @@ def tile_binarymlp_pa_kernel(tc, z0, g0, beta0, Wb1, bb1, out):
                     quantised += 2
             binarised = run_of_units(binarised)
             for m in range(OPEN_TILES, ROW_TILES):
-                for g in range(PASSES):
-                    one_pass(j, m, g)
-                bias_and_store(j, m)
+                pieces = 2 if (j, m) == (N_TILES - 1, ROW_TILES - 1) else 1
+                for first in range(0, N_TILE, N_TILE // pieces):
+                    for g in range(PASSES):
+                        one_pass(j, m, g, first, N_TILE // pieces)
+                    bias_and_store(j, m, first, N_TILE // pieces)
                 if quantised < binarised:
                     quantise_w(quantised // UNITS_PER_N_TILE, (quantised % UNITS_PER_N_TILE) // 2)
                     quantised += 2

from contextlib import ExitStack

import concourse.mybir as mybir
from concourse.masks import make_identity

F32 = mybir.dt.float32
BF16 = mybir.dt.bfloat16
U32 = mybir.dt.uint32
U8 = mybir.dt.uint8
FP8X4 = mybir.dt.float8_e4m3fn_x4
ALU = mybir.AluOpType
ACT = mybir.ActivationFunctionType

P = 128
PACK = 4
K_PASS = P * PACK
BATCH = 1024
K = 2048
N = 2048
PASSES = K // K_PASS
ROW_TILES = BATCH // P
HALF = BATCH // 2
N_TILE = 512
N_TILES = N // N_TILE
W_ROWS = 256
W_LOADS = N // W_ROWS
W_UNITS = W_LOADS * PASSES
UNITS_PER_N_TILE = W_UNITS // N_TILES
BN_CHUNK = 512
BN_EPS = 1e-5
PAIRS = K // (2 * P)
PSUM_BANKS = 8
Z_BANKS = 6
SUM_SLOTS = 4
VECTOR_STAT_PAIRS = 2
SUM_BANK = 6
UNIT_BANK = 7
LATE_UNIT_BANKS = (7, 4, 5, 6)
OPEN_TILES = 4
EARLY_UNIT_STEPS = (4, 6)
ACC_BANKS = (0, 1, 2, 3)
W_BANKS = (4, 5, 6, 7)
UNIT_RUN = 4
UNIT_EVERY = 4

SIGN_SCALE = 2.0**64
SIGN_BIAS = 2.0**-100

FLOPS = 2 * BATCH * K * N


def tile_binarymlp_pa_kernel(tc, z0, g0, beta0, Wb1, bb1, out):
    nc = tc.nc
    with ExitStack() as ctx:
        ctx.enter_context(tc.manual_schedule())
        const = ctx.enter_context(tc.tile_pool(name="const", bufs=1))
        inputs = ctx.enter_context(tc.tile_pool(name="inputs", bufs=1))
        keep = ctx.enter_context(tc.tile_pool(name="keep", bufs=1))
        small = ctx.enter_context(tc.tile_pool(name="small", bufs=4))
        h_stage = ctx.enter_context(tc.tile_pool(name="h_stage", bufs=2))
        w_stage = ctx.enter_context(tc.tile_pool(name="w_stage", bufs=PASSES))
        psum = ctx.enter_context(tc.psum_pool(name="psum", bufs=1))
        o_stage = ctx.enter_context(tc.tile_pool(name="o_stage", bufs=6))
        junk = ctx.enter_context(tc.tile_pool(name="junk", bufs=2))

        ident_bf = const.tile([P, P], BF16)
        make_identity(nc, ident_bf[:])
        ident_f32 = const.tile([P, P], F32)
        make_identity(nc, ident_f32[:])
        ones_bf = const.tile([P, P], BF16)
        nc.vector.memset(ones_bf[:], 1.0)
        gain_mean = const.tile([P, PAIRS, 2, 2], F32)
        zero_shift = const.tile([P, PAIRS, 2, 2], F32)
        nc.gpsimd.memset(zero_shift[:], 0.0)
        neg_gain = const.tile([P, PAIRS, 2], F32)

        vec_rows = const.tile([P, P], F32)
        nc.vector.memset(vec_rows[:], 0.0)
        z_sb = [inputs.tile([P, ROW_TILES, 2 * P], BF16, name="z_sb%d" % pair) for pair in range(PAIRS)]
        w_sb = [inputs.tile([P, W_ROWS // P, K], BF16, name="w_sb%d" % c) for c in range(W_LOADS)]

        def load_z(pair):
            nc.sync.dma_start(
                out=z_sb[pair][:],
                in_=z0[:, pair * 2 * P : (pair + 1) * 2 * P].rearrange("(r p) c -> p r c", p=P),
            )

        def load_w(c):
            nc.sync.dma_start(
                out=w_sb[c][:],
                in_=Wb1[c * W_ROWS : (c + 1) * W_ROWS, :].rearrange("(i p) k -> p i k", p=P),
            )

        load_z(0)
        nc.sync.dma_start(
            out=vec_rows[0:PAIRS, :].bitcast(BF16), in_=g0.rearrange("(c w) -> c w", c=PAIRS)
        )
        nc.sync.dma_start(
            out=vec_rows[PAIRS : 2 * PAIRS, :].bitcast(BF16), in_=beta0.rearrange("(c w) -> c w", c=PAIRS)
        )
        for pair in range(1, 4):
            load_z(pair)
        for c in range(N_TILE // W_ROWS):
            load_w(c)
            load_z(4 + 2 * c)
            load_z(5 + 2 * c)
        for c in range(N_TILE // W_ROWS, W_LOADS):
            load_w(c)
        bias_bc = const.tile([P, N], BF16)
        nc.sync.dma_start(out=bias_bc[:], in_=bb1.partition_broadcast(P))

        h_codes = keep.tile([P, PASSES, BATCH], U32, align_bytes=64)
        h_scales = keep.tile([P, PASSES, BATCH], U8, align_bytes=64)
        w_codes = keep.tile([P, PASSES, N], U32, align_bytes=64)
        w_scales = keep.tile([P, PASSES, N], U8, align_bytes=64)

        z_t_of = {}
        neg_mean_of = {}
        sq_sum_of = {}
        h_grouped_of = {}
        rstd_of = {}
        std_of = {}
        mean_var_of = {}
        scale_offset_of = {}
        h_t_of = {}
        w_grouped_of = {}
        w_t_of = {}
        acc_of = {}

        def transposes_z(pair):
            columns = z_sb[pair][:].rearrange("p r (q e) -> p r e q", e=2)
            for e in range(2):
                z_t = psum.tile([P, BATCH], BF16, tag="bank%d" % ((2 * pair + e) % Z_BANKS))
                for r in range(ROW_TILES):
                    nc.tensor.transpose(z_t[:, r * P : (r + 1) * P], columns[:, r, e, :], ident_bf[:])
                z_t_of[(pair, e)] = z_t

        def column_sums(pair, sums):
            columns = z_sb[pair][:].rearrange("p r (q e) -> p r e q", e=2)
            for e in range(2):
                for r in range(ROW_TILES):
                    nc.tensor.matmul(
                        out=sums[:, (2 * pair + e) % SUM_SLOTS, :],
                        lhsT=columns[:, r, e, :],
                        rhs=ones_bf[:],
                        start=(r == 0),
                        stop=(r == ROW_TILES - 1),
                    )

        def negative_mean(pair, sums):
            first = (2 * pair) % SUM_SLOTS
            neg_mean_of[pair] = small.tile([P, 2], F32, name="neg_mean")
            nc.scalar.activation(
                out=neg_mean_of[pair][:], in_=sums[:, first : first + 2, 0], func=ACT.Copy, scale=-1.0 / BATCH
            )

        def squares(pair):
            sq_sum_of[pair] = small.tile([P, 2], F32, name="sq_sum")
            for e in range(2):
                squared = junk.tile([P, BATCH], BF16)
                nc.scalar.activation(
                    out=squared[:],
                    in_=z_t_of[(pair, e)][:],
                    func=ACT.Square,
                    bias=neg_mean_of[pair][:, e : e + 1],
                    scale=1.0,
                    accum_out=sq_sum_of[pair][:, e : e + 1],
                )

        def vector_statistics(pair, between):
            stats = small.tile([P, 2, BATCH // BN_CHUNK, 6], F32)
            for e in range(2):
                for c in range(BATCH // BN_CHUNK):
                    nc.vector.bn_stats(
                        out=stats[:, e, c, :], in_=z_t_of[(pair, e)][:, c * BN_CHUNK : (c + 1) * BN_CHUNK]
                    )
                if e == 0:
                    between()
            mean_var = small.tile([P, 2, 2], F32)
            for e in range(2):
                nc.vector.bn_aggr(out=mean_var[:, e, :], in_=stats[:, e, :, :].rearrange("p c s -> p (c s)"))
            return mean_var

        def mean_times_gain(pair, mean_like, gain_like):
            nc.gpsimd.tensor_tensor(out=gain_mean[:, pair, :, 1], in0=mean_like, in1=gain_like, op=ALU.mult)

        def inverse_std(pair, var_like, var_factor):
            std_of[pair] = small.tile([P, 2], F32, name="std")
            nc.scalar.activation(out=std_of[pair][:], in_=var_like, func=ACT.Sqrt, bias=BN_EPS, scale=var_factor)

        def reciprocal_std(pair):
            rstd_of[pair] = small.tile([P, 2], F32, name="rstd")
            nc.vector.reciprocal(out=rstd_of[pair][:], in_=std_of[pair][:])

        def scale_and_offset(pair):
            scale_offset_of[pair] = small.tile([P, 2, 2], F32, name="scale_offset")
            for e in range(2):
                nc.vector.scalar_tensor_tensor(
                    out=scale_offset_of[pair][:, e, :],
                    in0=gain_mean[:, pair, e, :],
                    scalar=rstd_of[pair][:, e : e + 1],
                    in1=zero_shift[:, pair, e, :],
                    op0=ALU.mult,
                    op1=ALU.add,
                )

        def norm(pair):
            g, u = divmod(pair, 2)
            if u == 0:
                h_t_of[g] = h_stage.tile([P, PACK, BATCH], BF16, name="h_t")
            for e in range(2):
                nc.vector.tensor_scalar(
                    out=h_t_of[g][:, 2 * u + e, :],
                    in0=z_t_of[(pair, e)][:],
                    scalar1=scale_offset_of[pair][:, e, 0:1],
                    scalar2=scale_offset_of[pair][:, e, 1:2],
                    op0=ALU.mult,
                    op1=ALU.add,
                )

        def relu_grouped(g):
            h_grouped_of[g] = h_stage.tile([P, BATCH, PACK], BF16, align_bytes=64, name="h_grouped")
            nc.vector.tensor_scalar(
                out=h_grouped_of[g][:].rearrange("p (c i) t -> p c t i", i=4),
                in0=h_t_of[g][:].rearrange("p t (c i) -> p c t i", i=4),
                scalar1=0.0,
                scalar2=None,
                op0=ALU.max,
            )

        def quantise_h(g):
            nc.vector.quantize_mx(
                out=h_codes[:, g, :].bitcast(FP8X4),
                scales=h_scales[:, g, :],
                in_=h_grouped_of[g][:].rearrange("p b t -> p (b t)"),
            )

        def transposes_w(unit, bank):
            c, g = divmod(unit, PASSES)
            words = w_sb[c][:].bitcast(F32)
            w_t = psum.tile([P, 2, W_ROWS], F32, tag="bank%d" % bank)
            for u in range(2):
                first = (K_PASS // 2) * g + P * u
                for i in range(W_ROWS // P):
                    nc.tensor.transpose(
                        w_t[:, u, i * P : (i + 1) * P], words[:, i, first : first + P], ident_f32[:]
                    )
            w_t_of[unit] = w_t

        def sign_w(unit):
            w_t = w_t_of[unit]
            c, g = divmod(unit, PASSES)
            j, half = divmod(c, N_TILE // W_ROWS)
            if half == 0:
                w_grouped_of[(j, g)] = w_stage.tile([P, N_TILE, PACK], BF16, align_bytes=64, name="w_grouped")
            nc.scalar.activation(
                out=w_grouped_of[(j, g)][:, half * W_ROWS : (half + 1) * W_ROWS, :].rearrange(
                    "p r (u e) -> p r u e", e=2
                ),
                in_=w_t[:].bitcast(BF16).rearrange("p u (r e) -> p r u e", e=2),
                func=ACT.Sign,
                bias=SIGN_BIAS,
                scale=SIGN_SCALE,
            )

        def quantise_w(j, g):
            n_cols = slice(j * N_TILE, (j + 1) * N_TILE)
            nc.vector.quantize_mx(
                out=w_codes[:, g, n_cols].bitcast(FP8X4),
                scales=w_scales[:, g, n_cols],
                in_=w_grouped_of[(j, g)][:].rearrange("p r t -> p (r t)"),
            )

        def one_pass(j, m, g, first=0, width=N_TILE):
            if g == 0:
                acc = psum.tile([P, width], F32, tag="bank%d" % ACC_BANKS[(m + first // width) % len(ACC_BANKS)])
                acc_of[(j, m, first)] = acc
            m_cols = slice(m * P, (m + 1) * P)
            n_cols = slice(j * N_TILE + first, j * N_TILE + first + width)
            nc.tensor.matmul_mx(
                out=acc_of[(j, m, first)][:],
                lhsT=h_codes[:, g, m_cols].bitcast(FP8X4),
                lhsT_scale=h_scales[:, g, m_cols],
                rhs=w_codes[:, g, n_cols].bitcast(FP8X4),
                rhs_scale=w_scales[:, g, n_cols],
                start=(g == 0),
                stop=(g == PASSES - 1),
            )

        def bias_and_store(j, m, first=0, width=N_TILE):
            m_cols = slice(m * P, (m + 1) * P)
            n_cols = slice(j * N_TILE + first, j * N_TILE + first + width)
            result = o_stage.tile([P, N_TILE], F32)
            nc.vector.tensor_tensor(
                out=result[:, 0:width], in0=acc_of[(j, m, first)][:], in1=bias_bc[:, n_cols], op=ALU.add
            )
            nc.sync.dma_start(out=out[m_cols, n_cols], in_=result[:, 0:width])

        gain_shift = const.tile([P, 2 * PAIRS], F32)
        sums = psum.tile([P, SUM_SLOTS, P], F32, tag="bank%d" % SUM_BANK)
        unit_order = [
            PASSES * ((N_TILE // W_ROWS) * j + half) + g
            for j in range(N_TILES)
            for g in range(PASSES)
            for half in range(N_TILE // W_ROWS)
        ]
        first_units = unit_order[0:UNITS_PER_N_TILE]
        signed = []
        vec_t = psum.tile([P, P], F32, tag="bank%d" % UNIT_BANK)

        def spread_gain_and_shift():
            nc.vector.tensor_copy(out=gain_shift[:], in_=vec_t[:, 0 : 2 * PAIRS])
            gain = gain_shift[:, 0:PAIRS].bitcast(BF16).rearrange("p (c e) -> p c e", e=2)
            shift = gain_shift[:, PAIRS : 2 * PAIRS].bitcast(BF16).rearrange("p (c e) -> p c e", e=2)
            nc.gpsimd.tensor_copy(out=gain_mean[:, :, :, 0], in_=gain)
            nc.gpsimd.tensor_scalar(out=neg_gain[:], in0=gain, scalar1=-1.0, scalar2=0.0, op0=ALU.mult, op1=ALU.add)
            nc.gpsimd.tensor_copy(out=zero_shift[:, :, :, 1], in_=shift)

        def nothing():
            return None

        for step in range(PAIRS + 2):
            if step < PAIRS:
                transposes_z(step)
            if step == 0:
                nc.tensor.transpose(vec_t[:], vec_rows[:], ident_f32[:])
            if step < VECTOR_STAT_PAIRS:
                mean_var_of[step] = vector_statistics(step, spread_gain_and_shift if step == 0 else nothing)
                mean_times_gain(step, mean_var_of[step][:, :, 0], neg_gain[:, step, :])
            elif step < PAIRS:
                squares(step)
                inverse_std(step, sq_sum_of[step][:], 1.0 / BATCH)
            if 0 <= step - 1 < VECTOR_STAT_PAIRS:
                inverse_std(step - 1, mean_var_of[step - 1][:, :, 1], 1.0)
            if VECTOR_STAT_PAIRS <= step + 1 < PAIRS:
                column_sums(step + 1, sums)
                negative_mean(step + 1, sums)
                mean_times_gain(step + 1, neg_mean_of[step + 1][:], gain_mean[:, step + 1, :, 0])
            if step in EARLY_UNIT_STEPS:
                unit = first_units[len(signed)]
                transposes_w(unit, UNIT_BANK)
                sign_w(unit)
                signed.append(unit)
            if step == PAIRS:
                for unit in unit_order[len(signed) : UNITS_PER_N_TILE + UNIT_RUN]:
                    transposes_w(unit, LATE_UNIT_BANKS[(len(signed) - len(EARLY_UNIT_STEPS)) % len(LATE_UNIT_BANKS)])
                    sign_w(unit)
                    signed.append(unit)
            if 0 <= step - 2 < PAIRS:
                scale_and_offset(step - 2)
                norm(step - 2)
            if 0 <= step - 1 < PAIRS:
                reciprocal_std(step - 1)
            g, u = divmod(step - 2, 2)
            if 0 <= g < PASSES - 1 and u == 1:
                relu_grouped(g)
            g, u = divmod(step - 3, 2)
            if 0 <= g < PASSES - 1 and u == 1:
                quantise_h(g)
        quantise_w(0, 0)
        for m in range(OPEN_TILES):
            one_pass(0, m, 0)
        relu_grouped(PASSES - 1)
        quantise_w(0, 1)
        for m in range(OPEN_TILES):
            one_pass(0, m, 1)
        quantise_h(PASSES - 1)
        quantise_w(0, 2)
        for m in range(OPEN_TILES):
            one_pass(0, m, 2)
        quantise_w(0, 3)
        for m in range(OPEN_TILES):
            one_pass(0, m, 3)

        binarised = len(signed)
        quantised = UNITS_PER_N_TILE

        def run_of_units(first):
            for position in range(first, min(first + UNIT_RUN, W_UNITS)):
                transposes_w(unit_order[position], LATE_UNIT_BANKS[(position - len(EARLY_UNIT_STEPS)) % len(LATE_UNIT_BANKS)])
                sign_w(unit_order[position])
            return min(first + UNIT_RUN, W_UNITS)

        for j in range(N_TILES):
            if j > 0:
                binarised = run_of_units(binarised)
                for g in range(PASSES):
                    for m in range(OPEN_TILES):
                        one_pass(j, m, g)
            for m in range(OPEN_TILES):
                bias_and_store(j, m)
                if quantised < binarised:
                    quantise_w(quantised // UNITS_PER_N_TILE, (quantised % UNITS_PER_N_TILE) // 2)
                    quantised += 2
            binarised = run_of_units(binarised)
            for m in range(OPEN_TILES, ROW_TILES):
                pieces = 2 if (j, m) == (N_TILES - 1, ROW_TILES - 1) else 1
                for first in range(0, N_TILE, N_TILE // pieces):
                    for g in range(PASSES):
                        one_pass(j, m, g, first, N_TILE // pieces)
                    bias_and_store(j, m, first, N_TILE // pieces)
                if quantised < binarised:
                    quantise_w(quantised // UNITS_PER_N_TILE, (quantised % UNITS_PER_N_TILE) // 2)
                    quantised += 2
